import numpy as np
import ml_dtypes


def mxq(x, axis, fmt="e4m3"):
    dtype, down = {"e4m3": (ml_dtypes.float8_e4m3fn, 7), "e5m2": (ml_dtypes.float8_e5m2, 14)}[fmt]
    v = np.moveaxis(np.asarray(x, np.float32).astype(ml_dtypes.bfloat16).astype(np.float64), axis, -1)
    blocks = v.reshape(v.shape[:-1] + (-1, 32))
    amax = np.abs(blocks).max(-1, keepdims=True)
    byte = np.maximum(np.where(amax > 0, np.frexp(amax)[1] - 1 + 127, 0) - down, 1)
    scale = np.exp2(byte - 127.0)
    codes = (blocks / scale).astype(np.float32).astype(dtype).astype(np.float64)
    return np.moveaxis((codes * scale).reshape(v.shape), -1, axis)


WIDE = False


def mx_kscale(k):
    if not WIDE:
        return np.ones(k)
    levels = np.array([10, -10, 5, -5, 0])
    if k % 512:
        return np.exp2(np.random.permutation(np.resize(levels, k // 32))).repeat(32)
    a = np.empty((k // 512, 16))
    for p in range(k // 512):
        a[p, :8] = np.random.permutation(np.resize(levels, 8))
        for g in range(8):
            far = levels[np.abs(levels - a[p, g]) >= 10]
            a[p, g + 8] = far[np.random.randint(len(far))]
    return np.exp2(a.ravel()).repeat(32)


BF16 = ml_dtypes.bfloat16


def bf(x):
    return np.asarray(x, np.float32).astype(BF16)


def f64(x):
    return np.asarray(x).astype(np.float64)


N, ND, NP, KW = 256, 512, 6, 3
JW = KW - 1
KX = JW * ND


def windows(x):
    return np.moveaxis(x.reshape(N, ND, NP, JW), 1, -1).reshape(N, NP, KX)


def taps(W):
    return W.transpose(2, 1, 0).reshape(KW * ND, ND)


def draw0():
    s, t, u = mx_kscale(KX), mx_kscale(ND), mx_kscale(ND)
    r2 = np.concatenate([s, t]).reshape(KW, ND).T
    r3 = np.concatenate([s, u]).reshape(KW, ND).T
    c = 1.0 / np.sqrt(KW * ND)
    return {'x': bf(np.random.standard_normal((N, ND, JW * NP)) * np.tile(s.reshape(JW, ND).T, (1, NP))),
            'd_h1': bf(np.maximum(np.random.standard_normal((N, ND, NP)), 0.0) * t[:, None]),
            'd1': bf(np.random.standard_normal((N, ND, NP))),
            'W2': bf(np.random.standard_normal((ND, ND, KW)) * c * u[:, None, None] / r2[None]),
            'b2': bf(np.random.standard_normal(ND) * 0.3 * u),
            'W3': bf(np.random.standard_normal((ND, ND, KW)) * c / r3[None]),
            'b3': bf(np.random.standard_normal(ND) * 0.3)}


def core(x, d_h1, d1, W2, b2, W3, b3):
    xq = mxq(windows(f64(x)), 2, 'e4m3')
    w2, w3 = taps(f64(W2)), taps(f64(W3))
    a2 = (xq @ mxq(w2[:KX], 0, 'e4m3')) + (mxq(f64(d_h1).transpose(0, 2, 1), 2, 'e4m3') @ mxq(w2[KX:], 0, 'e4m3')) + f64(b2)
    h2 = np.maximum(a2, 0.0)
    a3 = (xq @ mxq(w3[:KX], 0, 'e4m3')) + (mxq(h2, 2, 'e4m3') @ mxq(w3[KX:], 0, 'e4m3')) + f64(b3)
    return np.maximum(a3.transpose(0, 2, 1) + f64(d1), 0.0)


def e4m3fn_bytes(y):
    return np.clip(np.asarray(y, np.float64), -448.0, 448.0).astype(np.float32).astype(ml_dtypes.float8_e4m3fn).view(np.uint8)


def e4m3fn_values(b):
    return np.asarray(b, np.uint8).view(ml_dtypes.float8_e4m3fn).astype(np.float64)


def setup_inputs():
    d = draw0()
    x0 = np.asarray(d['d_h1']).astype(np.float64)
    s = (np.max(np.abs(x0), axis=(0, 2), keepdims=True) / 448.0).astype(np.float32)
    out = {}
    for k, v in d.items():
        if k == 'd_h1':
            out['d_h1_bytes'] = e4m3fn_bytes(x0 / s.astype(np.float64))
            out['d_h1_scale'] = s
        else:
            out[k] = v
    return out


def reference(x, d_h1_bytes, d_h1_scale, d1, W2, b2, W3, b3):
    return core(x, e4m3fn_values(d_h1_bytes) * d_h1_scale.astype(np.float64), d1, W2, b2, W3, b3)

@@ -1,0 +1,283 @@
+from contextlib import ExitStack
+
+import concourse.mybir as mybir
+from concourse.masks import make_identity
+
+F32 = mybir.dt.float32
+BF16 = mybir.dt.bfloat16
+U8 = mybir.dt.uint8
+U32 = mybir.dt.uint32
+FP8 = mybir.dt.float8_e4m3fn
+FP8X4 = mybir.dt.float8_e4m3fn_x4
+ADD = mybir.AluOpType.add
+MULT = mybir.AluOpType.mult
+RELU = mybir.ActivationFunctionType.Relu
+
+P = 128
+N, ND, NP, KW = 256, 512, 6, 3
+JETS = 2 * NP
+FLOPS = 2 * 2 * N * NP * KW * ND * ND
+
+
+def tile_dijetresnetblock_pa_kernel(tc, x, d_h1_bytes, d_h1_scale, d1, W2, b2, W3, b3, out):
+    nc = tc.nc
+    with ExitStack() as ctx:
+        keep = ctx.enter_context(tc.tile_pool(name="keep", bufs=1))
+        work = ctx.enter_context(tc.tile_pool(name="work", bufs=2))
+        ptr = ctx.enter_context(tc.psum_pool(name="ptr", bufs=3))
+        pdj = ctx.enter_context(tc.psum_pool(name="pdj", bufs=1))
+        ps2 = ctx.enter_context(tc.psum_pool(name="ps2", bufs=2))
+        ps3 = ctx.enter_context(tc.psum_pool(name="ps3", bufs=2))
+        ctx.enter_context(tc.manual_schedule())
+
+        w2_raw = keep.tile([P, 4, ND * KW], BF16, name="w2_raw")
+        w3_raw = keep.tile([P, 4, ND * KW], BF16, name="w3_raw")
+        w2_src = W2.rearrange("(m t) i k -> m t (i k)", t=4)
+        w3_src = W3.rearrange("(t m) i k -> m t (i k)", t=4)
+        x_raw = [keep.tile([P, ND * JETS], BF16, name="x_raw%d" % b) for b in range(2)]
+        d_byt = [keep.tile([P, ND * NP], U8, name="d_byt%d" % b) for b in range(2)]
+        d_raw = [keep.tile([P, ND * NP], BF16, name="d_raw%d" % b) for b in range(2)]
+        d1_raw = [keep.tile([P, ND, NP], BF16, name="d1_raw%d" % b) for b in range(2)]
+        res = [keep.tile([P, ND, NP], F32, name="res%d" % b) for b in range(2)]
+        sc = keep.tile([P, 4], F32, name="sc")
+        b2t = keep.tile([P, 4], BF16, name="b2t")
+        b3t = keep.tile([P, ND], BF16, name="b3t")
+        rows = [slice(b * P, (b + 1) * P) for b in range(2)]
+
+        for t in range(4):
+            nc.sync.dma_start(out=w2_raw[:, t, :], in_=w2_src[:, t, :])
+        nc.sync.dma_start(out=x_raw[0][:], in_=x[rows[0]].rearrange("b i j -> b (i j)"))
+        nc.sync.dma_start(out=d_byt[0][:], in_=d_h1_bytes[rows[0]].rearrange("b i s -> b (i s)"))
+        nc.sync.dma_start(out=sc[:], in_=d_h1_scale.rearrange("o (p t) w -> p (o t w)", t=4))
+        nc.sync.dma_start(out=b2t[:], in_=b2.rearrange("(p t) -> p t", t=4))
+        for t in range(4):
+            nc.sync.dma_start(out=w3_raw[:, t, :], in_=w3_src[:, t, :])
+        nc.sync.dma_start(out=x_raw[1][:], in_=x[rows[1]].rearrange("b i j -> b (i j)"))
+        nc.sync.dma_start(out=d_byt[1][:], in_=d_h1_bytes[rows[1]].rearrange("b i s -> b (i s)"))
+        nc.sync.dma_start(out=b3t[:], in_=b3.partition_broadcast(P))
+        for b in range(2):
+            nc.sync.dma_start(out=d1_raw[b][:], in_=d1[rows[b]])
+
+        ident = keep.tile([P, P], BF16, name="ident")
+        make_identity(nc, ident[:])
+        warm = keep.tile([P, 1], F32, name="warm")
+        nc.vector.memset(warm[:], 0.0)
+        nc.scalar.activation(out=warm[:], in_=warm[:], func=RELU)
+
+        OC = 64
+        for b in range(2):
+            for o in range(0, ND, OC):
+                nc.gpsimd.tensor_tensor(
+                    out=res[b][:, o : o + OC, :], in0=d1_raw[b][:, o : o + OC, :],
+                    in1=b3t[:, o : o + OC].unsqueeze(2).to_broadcast([P, OC, NP]), op=ADD)
+
+        ORDER = [(0, 0), (0, 1), (0, 2), (1, 2), (1, 0), (1, 1), (2, 0), (2, 1), (2, 2), (3, 2), (3, 0), (3, 1)]
+        POS = {g: n for n, g in enumerate(ORDER)}
+        w2_g = keep.tile([P, 12, P, 4], BF16, name="w2_g", align_bytes=64)
+        w2_c = keep.tile([P, 12, P], U32, name="w2_c", align_bytes=64)
+        w2_s = keep.tile([P, 12, P], U8, name="w2_s", align_bytes=64)
+        w3_g = keep.tile([P, 3, ND, 4], BF16, name="w3_g", align_bytes=64)
+        w3_c = keep.tile([P, 3, ND], U32, name="w3_c", align_bytes=64)
+        w3_s = keep.tile([P, 3, ND], U8, name="w3_s", align_bytes=64)
+
+        def weight_transposes(raw, j):
+            bank = ptr.tile([P, 2, 4, P], BF16, name="bank")
+            for n in range(2):
+                o, k = ORDER[2 * j + n]
+                view = raw[:, o, :].rearrange("m (p t k) -> m t k p", t=4, k=KW)
+                for t in range(4):
+                    nc.tensor.transpose(bank[:, n, t, :], view[:, t, k, :], ident[:])
+            return bank
+
+        def copy(engine, out_ap, in_ap):
+            if engine == "S":
+                nc.scalar.copy(out=out_ap, in_=in_ap)
+            else:
+                nc.vector.tensor_copy(out=out_ap, in_=in_ap)
+
+        def w2_copy(bank, j, engine):
+            copy(engine, w2_g[:, 2 * j : 2 * j + 2, :, :], bank[:].rearrange("p n t m -> p n m t"))
+
+        def w2_quant(j):
+            g = slice(2 * j, 2 * j + 2)
+            nc.vector.quantize_mx(
+                out=w2_c[:, g, :].rearrange("p n m -> p (n m)").bitcast(FP8X4),
+                scales=w2_s[:, g, :].rearrange("p n m -> p (n m)"),
+                in_=w2_g[:, g, :, :].rearrange("p n m t -> p (n m t)"))
+
+        def w3_copy(bank, j, engine):
+            (oa, ka), (ob, kb) = ORDER[2 * j], ORDER[2 * j + 1]
+            src = bank[:].rearrange("p n t m -> p n m t")
+            if oa == ob:
+                copy(engine, w3_g[:, ka : ka + 2, oa * P : (oa + 1) * P, :], src)
+            else:
+                dst = w3_g[:, ka, oa * P : (oa + 2) * P, :].rearrange("p (n m) t -> p n m t", n=2)
+                copy(engine, dst, src)
+
+        def w3_quant(k, half):
+            g = slice(half * 256, half * 256 + 256)
+            nc.vector.quantize_mx(out=w3_c[:, k, g].bitcast(FP8X4), scales=w3_s[:, k, g],
+                                  in_=w3_g[:, k, g, :].rearrange("p m t -> p (m t)"))
+
+        x_g, x_c, x_s, d_g, d_c, d_s, h_g, h_c, h_s = [], [], [], [], [], [], [], [], []
+        for q in range(6):
+            x_g.append(work.tile([P, 2, 2, P, 4], BF16, name="x_g", align_bytes=64) if q < 0 else None)
+            x_c.append(keep.tile([P, 2, 2, P], U32, name="x_c%d" % q, align_bytes=64))
+            x_s.append(keep.tile([P, 2, 2, P], U8, name="x_s%d" % q, align_bytes=64))
+            d_g.append(None)
+            d_c.append(keep.tile([P, 2, P], U32, name="d_c%d" % q, align_bytes=64))
+            d_s.append(keep.tile([P, 2, P], U8, name="d_s%d" % q, align_bytes=64))
+            h_g.append(None)
+            h_c.append(keep.tile([P, 2, P], U32, name="h_c%d" % q, align_bytes=64))
+            h_s.append(keep.tile([P, 2, P], U8, name="h_s%d" % q, align_bytes=64))
+        d_bank = {}
+
+        def slot_transposes(n):
+            b, s, q, h = n // 6, n % 6, n // 2, n % 2
+            bank = ptr.tile([P, 2, 4, P], BF16, name="bank")
+            xv = x_raw[b][:].rearrange("b (p t j) -> b t j p", t=4, j=JETS)
+            for k in range(2):
+                for t in range(4):
+                    nc.tensor.transpose(bank[:, k, t, :], xv[:, t, 2 * s + k, :], ident[:])
+            if h == 0:
+                d_bank[q] = pdj.tile([P, 2, 4, P], BF16, name="dbank")
+            dv = d_raw[b][:].rearrange("b (p t s) -> b t s p", t=4, s=NP)
+            for t in range(4):
+                nc.tensor.transpose(d_bank[q][:, h, t, :], dv[:, t, s, :], ident[:])
+            return bank
+
+        def slot_copy(bank, n, engine):
+            q, h = n // 2, n % 2
+            if h == 0:
+                x_g[q] = work.tile([P, 2, 2, P, 4], BF16, name="xg", align_bytes=64)
+            copy(engine, x_g[q][:, h], bank[:].rearrange("p k t b -> p k b t"))
+
+        def dijet_copy(q):
+            d_g[q] = work.tile([P, 2, P, 4], BF16, name="dg", align_bytes=64)
+            nc.vector.tensor_tensor(
+                out=d_g[q][:], in0=d_bank[q][:].rearrange("p s t b -> p s b t"),
+                in1=sc[:].unsqueeze(1).unsqueeze(1).to_broadcast([P, 2, P, 4]), op=MULT)
+
+        def x_quant(q):
+            nc.vector.quantize_mx(out=x_c[q][:].rearrange("p s k b -> p (s k b)").bitcast(FP8X4),
+                                  scales=x_s[q][:].rearrange("p s k b -> p (s k b)"),
+                                  in_=x_g[q][:].rearrange("p s k b t -> p (s k b t)"))
+
+        def d_quant(q):
+            nc.vector.quantize_mx(out=d_c[q][:].rearrange("p s b -> p (s b)").bitcast(FP8X4),
+                                  scales=d_s[q][:].rearrange("p s b -> p (s b)"),
+                                  in_=d_g[q][:].rearrange("p s b t -> p (s b t)"))
+
+        def stage2(n):
+            q, h = n // 2, n % 2
+            acc = ps2.tile([P, 4, P], F32, name="acc2")
+            for o in range(4):
+                for k in range(KW):
+                    g = POS[(o, k)]
+                    rhs = x_c[q][:, h, k, :] if k < 2 else d_c[q][:, h, :]
+                    rhs_s = x_s[q][:, h, k, :] if k < 2 else d_s[q][:, h, :]
+                    nc.tensor.matmul_mx(out=acc[:, o, :], lhsT=w2_c[:, g, :].bitcast(FP8X4), lhsT_scale=w2_s[:, g, :],
+                                        rhs=rhs.bitcast(FP8X4), rhs_scale=rhs_s, start=(k == 0), stop=(k == 2))
+            return acc
+
+        def h_copy(acc, n):
+            q, h = n // 2, n % 2
+            if h == 0:
+                h_g[q] = work.tile([P, 2, P, 4], BF16, name="hg", align_bytes=64)
+            nc.vector.tensor_tensor(out=h_g[q][:, h], in0=acc[:].rearrange("p t b -> p b t"),
+                                    in1=b2t[:].unsqueeze(1).to_broadcast([P, P, 4]), op=ADD)
+
+        def h_relu(q):
+            nc.vector.tensor_scalar_max(out=h_g[q][:], in0=h_g[q][:], scalar1=0.0)
+
+        def h_quant(q):
+            nc.vector.quantize_mx(out=h_c[q][:].rearrange("p s b -> p (s b)").bitcast(FP8X4),
+                                  scales=h_s[q][:].rearrange("p s b -> p (s b)"),
+                                  in_=h_g[q][:].rearrange("p s b t -> p (s b t)"))
+
+        def stage3(b, half, g):
+            acc = ps3.tile([P, 2, 256], F32, name="acc3")
+            o = slice(half * 256, half * 256 + 256)
+            q = b * 3 + g
+            for h in range(2):
+                for k in range(KW):
+                    lhs = x_c[q][:, h, k, :] if k < 2 else h_c[q][:, h, :]
+                    lhs_s = x_s[q][:, h, k, :] if k < 2 else h_s[q][:, h, :]
+                    nc.tensor.matmul_mx(out=acc[:, h, :], lhsT=lhs.bitcast(FP8X4), lhsT_scale=lhs_s,
+                                        rhs=w3_c[:, k, o].bitcast(FP8X4), rhs_scale=w3_s[:, k, o],
+                                        start=(k == 0), stop=(k == 2))
+            return acc
+
+        sums = {}
+
+        def add_res(acc, b, half, g):
+            if g == 0:
+                sums[b, half] = work.tile([P, 3, 256, 2], F32, name="sums")
+            nc.vector.tensor_tensor(
+                out=sums[b, half][:, g], in0=acc[:].rearrange("p s o -> p o s"),
+                in1=res[b][:, half * 256 : half * 256 + 256, 2 * g : 2 * g + 2], op=ADD)
+
+        def finish(b, half, o0, o1, engine):
+            fin = work.tile([P, o1 - o0, NP], F32, name="fin%d" % (o1 - o0))
+            dst = fin[:].rearrange("p o (g s) -> p o g s", s=2)
+            src = sums[b, half][:, :, o0:o1, :].rearrange("p g o s -> p o g s")
+            if engine == "S":
+                nc.scalar.activation(out=dst, in_=src, func=RELU)
+            else:
+                nc.vector.tensor_scalar_max(out=dst, in0=src, scalar1=0.0)
+            nc.sync.dma_start(out=out[rows[b], half * 256 + o0 : half * 256 + o1, :], in_=fin[:])
+
+        later = {}
+
+        def at(step, fn, *args):
+            later.setdefault(step, []).append((fn, args))
+
+        plan = [("W2", j) for j in range(6)]
+        plan += [("X", 0), ("X", 1), ("W3", 0), ("X", 2), ("W3", 1), ("X", 3), ("S2", 0), ("W3", 2), ("X", 4),
+                 ("S2", 1), ("W3", 3), ("X", 5), ("S2", 2), ("W3", 4), ("X", 6), ("S2", 3), ("W3", 5), ("X", 7),
+                 ("S2", 4), ("U", 0), ("X", 8), ("S2", 5), ("U", 1), ("X", 9), ("S2", 6), ("U", 2), ("X", 10),
+                 ("S2", 7), ("U", 3), ("X", 11), ("S2", 8), ("U", 4), ("S2", 9), ("U", 5), ("S2", 10), ("S2", 11)]
+        plan += [("U", j) for j in range(6, 12)]
+
+        for step, (kind, n) in enumerate(plan):
+            if kind == "W2":
+                bank = weight_transposes(w2_raw, n)
+                w2_copy(bank, n, "V" if n in (1, 4) else "S")
+                at(step + 1, w2_quant, n)
+            elif kind == "X":
+                if n == 0:
+                    nc.vector.tensor_copy(out=d_raw[0][:], in_=d_byt[0][:].bitcast(FP8))
+                if n == 4:
+                    nc.scalar.copy(out=d_raw[1][:], in_=d_byt[1][:].bitcast(FP8))
+                bank = slot_transposes(n)
+                slot_copy(bank, n, "S")
+                if n % 2 == 1:
+                    dijet_copy(n // 2)
+                    at(step + 1, x_quant, n // 2)
+                    at(step + 1, d_quant, n // 2)
+            elif kind == "W3":
+                bank = weight_transposes(w3_raw, n)
+                w3_copy(bank, n, "S")
+                if n % 3 == 2:
+                    for k in range(KW):
+                        at(step + 1, w3_quant, k, n // 3)
+            elif kind == "S2":
+                acc = stage2(n)
+                h_copy(acc, n)
+                if n % 2 == 1:
+                    at(step + 1, h_relu, n // 2)
+                    at(step + 2 if n < 11 else step + 1, h_quant, n // 2)
+            else:
+                b, half, g = n // 6, (n % 6) // 3, n % 3
+                acc = stage3(b, half, g)
+                add_res(acc, b, half, g)
+                if g == 2:
+                    if (b, half) == (1, 1):
+                        at(step + 1, finish, b, half, 0, 128, "S")
+                        at(step + 1, finish, b, half, 128, 256, "V")
+                    else:
+                        at(step + 1, finish, b, half, 0, 256, "S")
+            for fn, args in later.pop(step, []):
+                fn(*args)
+        for fn, args in later.pop(len(plan), []):
+            fn(*args)

@@ -17,6 +17,26 @@ P = 128
 N, ND, NP, KW = 256, 512, 6, 3
 JETS = 2 * NP
 FLOPS = 2 * 2 * N * NP * KW * ND * ND
+GROUPS = [(0, 0), (0, 1), (0, 2), (1, 2), (1, 0), (1, 1), (2, 0), (2, 1), (2, 2), (3, 2), (3, 0), (3, 1)]
+POS = {g: n for n, g in enumerate(GROUPS)}
+
+SEQ = """
+ws:V:0,0,0 ws:V:0,0,1 ws:V:0,1,0 wt:T:0,0 ws:V:0,2,0 wc:S:0,0 ws:V:0,1,1 ws:V:0,2,1 wt:T:0,1 ws:V:0,3,0
+wc:S:0,1 ws:V:0,3,1 w2q:V:0 wt:T:0,5 wt:T:0,3 wc:S:0,5 wt:T:0,4 wc:S:0,4 xt:T:0 wc:S:0,3 wid:V:0 xt:T:1 xc:S:0
+xt:T:5 xc:S:1 ws:V:1,0,1 ds:V:0,2 wt:T:0,2 ds:V:0,3 xc:S:5 w2q:V:2 xt:T:4 ds:V:0,1 ws:V:1,1,1 wc:S:0,2 xt:T:3
+xq:V:0 xc:S:4 ds:V:0,0 ws:V:1,0,0 dt:T:0 ws:V:1,1,0 xc:S:3 dc:V:0 wt:T:1,1 wt:T:1,0 wc:S:1,1 wt:T:1,2
+ws:V:1,3,0 wc:S:1,0 xt:T:2 dq:V:0 w2q:V:1 dt:T:1 ws:V:1,3,1 xc:S:2 ws:V:1,2,0 xt:T:6 dc:V:1 wc:S:1,2 S2:T:0,1
+ws:V:1,2,1 xc:S:6 r:G:1,0 dq:V:1 S2:T:0,0 xq:V:1 E:S:0,2 dt:T:2 E:S:0,0 wt:T:1,4 dc:V:2 wt:T:1,5 E:S:0,1
+wt:T:1,3 wc:S:1,4 S2:T:1,1 E:S:0,3 w3q:V:0,1 r:G:0,0 wc:S:1,3 w3q:V:0,0 S2:T:1,0 hi:V:0 E:S:1,2 wc:S:1,5
+xt:T:7 E:S:1,0 w3q:V:1,2 E:S:1,3 w3q:V:0,2 xt:T:8 E:S:1,1 w3q:V:1,1 wid:S:1 w3q:V:1,0 hq:V:0 r:G:0,1 xt:T:9
+hi:V:1 dq:V:2 xq:V:2 U:T:0 U:T:3 F:V:0 xc:S:7 S2:T:2,1 ds:V:1,2 r:G:0,2 ds:V:1,3 ds:V:1,0 S2:T:2,0 xc:S:9
+ds:V:1,1 hq:V:1 xq:V:3 dt:T:3 E:S:2,2 xt:T:10 E:S:2,0 dc:V:3 E:S:2,3 E:S:2,1 xt:T:11 r:G:1,2 F:V:3 dq:V:3
+dt:T:4 hi:V:2 xc:S:11 U:T:4 dc:V:4 S2:T:3,0 xc:S:8 hq:V:2 S2:T:3,1 dq:V:4 r:G:1,1 E:S:3,0 xq:V:4 dt:T:5
+E:S:3,2 U:T:2 E:S:3,1 dc:V:5 E:S:3,3 xc:S:10 S2:T:4,0 F:V:4 S2:T:4,1 dq:V:5 F:V:2 U:T:1 E:S:4,2 xq:V:5 E:S:4,0
+U:T:5 E:S:4,3 F:V:1 E:S:4,1 S2:T:5,1 hi:V:3 R:S:0,0,0,256 F:V:5 S2:T:5,0 hq:V:3 hi:V:4 U:T:6 E:S:5,2 E:S:5,0
+E:S:5,3 hq:V:4 E:S:5,1 F:V:6 U:T:7 R:S:0,1,0,256 hi:V:5 U:T:10 F:V:7 hq:V:5 U:T:9 F:V:10 U:T:11 F:V:9 U:T:8
+F:V:11 R:S:1,1,0,100 F:V:8 R:V:1,1,100,256 R:S:1,0,0,100 R:V:1,0,100,256
+"""
 
 
 def tile_dijetresnetblock_pa_kernel(tc, x, d_h1_bytes, d_h1_scale, d1, W2, b2, W3, b3, out):
@@ -30,64 +50,46 @@ def tile_dijetresnetblock_pa_kernel(tc, x, d_h1_bytes, d_h1_scale, d1, W2, b2, W
         ps3 = ctx.enter_context(tc.psum_pool(name="ps3", bufs=2))
         ctx.enter_context(tc.manual_schedule())
 
-        w2_raw = keep.tile([P, 4, ND * KW], BF16, name="w2_raw")
-        w3_raw = keep.tile([P, 4, ND * KW], BF16, name="w3_raw")
-        w2_src = W2.rearrange("(m t) i k -> m t (i k)", t=4)
-        w3_src = W3.rearrange("(t m) i k -> m t (i k)", t=4)
+        w_raw = [[keep.tile([P, 2, ND * KW], BF16, name="w_raw%d_%d" % (i, n), tag="raw%d_%d" % (i, n)) for n in range(2)] for i in range(2)]
+        w_src = [W2.rearrange("(m t) i k -> m t (i k)", t=4), W3.rearrange("(t m) i k -> m t (i k)", t=4)]
         x_raw = [keep.tile([P, ND * JETS], BF16, name="x_raw%d" % b) for b in range(2)]
         d_byt = [keep.tile([P, ND * NP], U8, name="d_byt%d" % b) for b in range(2)]
-        d_raw = [keep.tile([P, ND * NP], BF16, name="d_raw%d" % b) for b in range(2)]
-        d1_raw = [keep.tile([P, ND, NP], BF16, name="d1_raw%d" % b) for b in range(2)]
-        res = [keep.tile([P, ND, NP], F32, name="res%d" % b) for b in range(2)]
+        d_raw = [keep.tile([P, ND * NP], BF16, name="d_raw%d" % b, tag="d_raw") for b in range(2)]
+        d1_raw = [keep.tile([P, ND, NP], BF16, name="d1_raw%d" % b, tag="raw0_%d" % b) for b in range(2)]
+        res = [keep.tile([P, 3, ND, 2], F32, name="res%d" % b) for b in range(2)]
         sc = keep.tile([P, 4], F32, name="sc")
         b2t = keep.tile([P, 4], BF16, name="b2t")
         b3t = keep.tile([P, ND], BF16, name="b3t")
         rows = [slice(b * P, (b + 1) * P) for b in range(2)]
 
+        def load_w(i, t):
+            nc.sync.dma_start(out=w_raw[i][t // 2][:, t % 2, :], in_=w_src[i][:, t, :])
+
+        def load_x(b):
+            nc.sync.dma_start(out=x_raw[b][:], in_=x[rows[b]].rearrange("b i j -> b (i j)"))
+
+        def load_d(b):
+            nc.sync.dma_start(out=d_byt[b][:], in_=d_h1_bytes[rows[b]].rearrange("b i s -> b (i s)"))
+
         for t in range(4):
-            nc.sync.dma_start(out=w2_raw[:, t, :], in_=w2_src[:, t, :])
-        nc.sync.dma_start(out=x_raw[0][:], in_=x[rows[0]].rearrange("b i j -> b (i j)"))
-        nc.sync.dma_start(out=d_byt[0][:], in_=d_h1_bytes[rows[0]].rearrange("b i s -> b (i s)"))
+            load_w(0, t)
+        load_x(0)
+        load_d(0)
         nc.sync.dma_start(out=sc[:], in_=d_h1_scale.rearrange("o (p t) w -> p (o t w)", t=4))
         nc.sync.dma_start(out=b2t[:], in_=b2.rearrange("(p t) -> p t", t=4))
         for t in range(4):
-            nc.sync.dma_start(out=w3_raw[:, t, :], in_=w3_src[:, t, :])
-        nc.sync.dma_start(out=x_raw[1][:], in_=x[rows[1]].rearrange("b i j -> b (i j)"))
-        nc.sync.dma_start(out=d_byt[1][:], in_=d_h1_bytes[rows[1]].rearrange("b i s -> b (i s)"))
+            load_w(1, t)
+        load_d(1)
         nc.sync.dma_start(out=b3t[:], in_=b3.partition_broadcast(P))
-        for b in range(2):
-            nc.sync.dma_start(out=d1_raw[b][:], in_=d1[rows[b]])
+        nc.sync.dma_start(out=d1_raw[0][:], in_=d1[rows[0]])
+        load_x(1)
+        nc.sync.dma_start(out=d1_raw[1][:], in_=d1[rows[1]])
 
-        ident = keep.tile([P, P], BF16, name="ident")
+        ident = keep.tile([P, P], F32, name="ident")
         make_identity(nc, ident[:])
         warm = keep.tile([P, 1], F32, name="warm")
         nc.vector.memset(warm[:], 0.0)
         nc.scalar.activation(out=warm[:], in_=warm[:], func=RELU)
-
-        OC = 64
-        for b in range(2):
-            for o in range(0, ND, OC):
-                nc.gpsimd.tensor_tensor(
-                    out=res[b][:, o : o + OC, :], in0=d1_raw[b][:, o : o + OC, :],
-                    in1=b3t[:, o : o + OC].unsqueeze(2).to_broadcast([P, OC, NP]), op=ADD)
-
-        ORDER = [(0, 0), (0, 1), (0, 2), (1, 2), (1, 0), (1, 1), (2, 0), (2, 1), (2, 2), (3, 2), (3, 0), (3, 1)]
-        POS = {g: n for n, g in enumerate(ORDER)}
-        w2_g = keep.tile([P, 12, P, 4], BF16, name="w2_g", align_bytes=64)
-        w2_c = keep.tile([P, 12, P], U32, name="w2_c", align_bytes=64)
-        w2_s = keep.tile([P, 12, P], U8, name="w2_s", align_bytes=64)
-        w3_g = keep.tile([P, 3, ND, 4], BF16, name="w3_g", align_bytes=64)
-        w3_c = keep.tile([P, 3, ND], U32, name="w3_c", align_bytes=64)
-        w3_s = keep.tile([P, 3, ND], U8, name="w3_s", align_bytes=64)
-
-        def weight_transposes(raw, j):
-            bank = ptr.tile([P, 2, 4, P], BF16, name="bank")
-            for n in range(2):
-                o, k = ORDER[2 * j + n]
-                view = raw[:, o, :].rearrange("m (p t k) -> m t k p", t=4, k=KW)
-                for t in range(4):
-                    nc.tensor.transpose(bank[:, n, t, :], view[:, t, k, :], ident[:])
-            return bank
 
         def copy(engine, out_ap, in_ap):
             if engine == "S":
@@ -95,130 +97,158 @@ def tile_dijetresnetblock_pa_kernel(tc, x, d_h1_bytes, d_h1_scale, d1, W2, b2, W
             else:
                 nc.vector.tensor_copy(out=out_ap, in_=in_ap)
 
-        def w2_copy(bank, j, engine):
-            copy(engine, w2_g[:, 2 * j : 2 * j + 2, :, :], bank[:].rearrange("p n t m -> p n m t"))
+        OC = 64
 
-        def w2_quant(j):
-            g = slice(2 * j, 2 * j + 2)
-            nc.vector.quantize_mx(
-                out=w2_c[:, g, :].rearrange("p n m -> p (n m)").bitcast(FP8X4),
-                scales=w2_s[:, g, :].rearrange("p n m -> p (n m)"),
-                in_=w2_g[:, g, :, :].rearrange("p n m t -> p (n m t)"))
+        def residual(engine, b, g):
+            for o in range(0, ND, OC if engine == "G" else ND):
+                c = slice(o, o + (OC if engine == "G" else ND))
+                eng = nc.gpsimd if engine == "G" else nc.vector
+                eng.tensor_tensor(out=res[b][:, g, c, :], in0=d1_raw[b][:, c, 2 * g : 2 * g + 2],
+                                  in1=b3t[:, c].unsqueeze(2).to_broadcast([P, c.stop - c.start, 2]), op=ADD)
 
-        def w3_copy(bank, j, engine):
-            (oa, ka), (ob, kb) = ORDER[2 * j], ORDER[2 * j + 1]
-            src = bank[:].rearrange("p n t m -> p n m t")
+        w_sh = [[keep.tile([P, KW, 2, P, 2], BF16, name="w_sh%d_%d" % (i, o), tag="w_sh%d" % o) for o in range(4)] for i in range(2)]
+        w2_g = keep.tile([P, 12, P, 2], F32, name="w2_g", tag="w_g", align_bytes=64)
+        w2_c = keep.tile([P, 12, P], U32, name="w2_c", align_bytes=64)
+        w2_s = keep.tile([P, 12, P], U8, name="w2_s", align_bytes=64)
+        w3_g = keep.tile([P, KW, ND, 2], F32, name="w3_g", tag="w_g", align_bytes=64)
+        w3_c = keep.tile([P, KW, ND], U32, name="w3_c", align_bytes=64)
+        w3_s = keep.tile([P, KW, ND], U8, name="w3_s", align_bytes=64)
+        w_bank = {}
+
+        def w_shuffle(engine, i, o, u):
+            src = w_raw[i][o // 2][:, o % 2, :].rearrange("m (p u e k) -> m u p k e", u=2, e=2, k=KW)
+            copy(engine, w_sh[i][o][:, :, u, :, :].rearrange("m k p e -> m p k e"), src[:, u])
+
+        def w_transpose(i, j):
+            bank = ptr.tile([P, 2, 2, P], F32, name="bank")
+            for n in range(2):
+                o, k = GROUPS[2 * j + n]
+                for u in range(2):
+                    nc.tensor.transpose(bank[:, n, u, :], w_sh[i][o][:, k, u].rearrange("m p e -> m (p e)").bitcast(F32), ident[:])
+            w_bank[i, j] = bank
+
+        def w_copy(engine, i, j):
+            src = w_bank[i, j][:].rearrange("p n u m -> p n m u")
+            if i == 0:
+                copy(engine, w2_g[:, 2 * j : 2 * j + 2], src)
+                return
+            (oa, ka), (ob, kb) = GROUPS[2 * j], GROUPS[2 * j + 1]
             if oa == ob:
                 copy(engine, w3_g[:, ka : ka + 2, oa * P : (oa + 1) * P, :], src)
             else:
-                dst = w3_g[:, ka, oa * P : (oa + 2) * P, :].rearrange("p (n m) t -> p n m t", n=2)
-                copy(engine, dst, src)
+                copy(engine, w3_g[:, ka, oa * P : (oa + 2) * P, :].rearrange("p (n m) u -> p n m u", n=2), src)
 
-        def w3_quant(k, half):
+        def w2_quant(j):
+            g = slice(4 * j, 4 * j + 4)
+            nc.vector.quantize_mx(
+                out=w2_c[:, g, :].rearrange("p n m -> p (n m)").bitcast(FP8X4),
+                scales=w2_s[:, g, :].rearrange("p n m -> p (n m)"),
+                in_=w2_g[:, g, :, :].rearrange("p n m u -> p (n m u)").bitcast(BF16))
+
+        def w3_quant(half, k):
             g = slice(half * 256, half * 256 + 256)
             nc.vector.quantize_mx(out=w3_c[:, k, g].bitcast(FP8X4), scales=w3_s[:, k, g],
-                                  in_=w3_g[:, k, g, :].rearrange("p m t -> p (m t)"))
+                                  in_=w3_g[:, k, g, :].rearrange("p m u -> p (m u)").bitcast(BF16))
 
-        x_g, x_c, x_s, d_g, d_c, d_s, h_g, h_c, h_s = [], [], [], [], [], [], [], [], []
-        for q in range(6):
-            x_g.append(work.tile([P, 2, 2, P, 4], BF16, name="x_g", align_bytes=64) if q < 0 else None)
-            x_c.append(keep.tile([P, 2, 2, P], U32, name="x_c%d" % q, align_bytes=64))
-            x_s.append(keep.tile([P, 2, 2, P], U8, name="x_s%d" % q, align_bytes=64))
-            d_g.append(None)
-            d_c.append(keep.tile([P, 2, P], U32, name="d_c%d" % q, align_bytes=64))
-            d_s.append(keep.tile([P, 2, P], U8, name="d_s%d" % q, align_bytes=64))
-            h_g.append(None)
-            h_c.append(keep.tile([P, 2, P], U32, name="h_c%d" % q, align_bytes=64))
-            h_s.append(keep.tile([P, 2, P], U8, name="h_s%d" % q, align_bytes=64))
-        d_bank = {}
+        x_c = [keep.tile([P, 2, 2, P], U32, name="x_c%d" % q, align_bytes=64) for q in range(6)]
+        x_s = [keep.tile([P, 2, 2, P], U8, name="x_s%d" % q, align_bytes=64) for q in range(6)]
+        d_c = [keep.tile([P, 2 * P], U32, name="d_c%d" % q, align_bytes=64) for q in range(6)]
+        d_s = [keep.tile([P, 2 * P], U8, name="d_s%d" % q, align_bytes=64) for q in range(6)]
+        h_c = [keep.tile([P, 2 * P], U32, name="h_c%d" % q, align_bytes=64) for q in range(6)]
+        h_s = [keep.tile([P, 2 * P], U8, name="h_s%d" % q, align_bytes=64) for q in range(6)]
+        d_sh = [keep.tile([P, 3, 4, P], F32, name="d_sh%d" % b) for b in range(2)]
+        x_bank, d_bank, x_g, d_g, acc2, h_p, h_g, acc3, sums = {}, {}, {}, {}, {}, {}, {}, {}, {}
 
-        def slot_transposes(n):
-            b, s, q, h = n // 6, n % 6, n // 2, n % 2
-            bank = ptr.tile([P, 2, 4, P], BF16, name="bank")
-            xv = x_raw[b][:].rearrange("b (p t j) -> b t j p", t=4, j=JETS)
-            for k in range(2):
-                for t in range(4):
-                    nc.tensor.transpose(bank[:, k, t, :], xv[:, t, 2 * s + k, :], ident[:])
-            if h == 0:
-                d_bank[q] = pdj.tile([P, 2, 4, P], BF16, name="dbank")
-            dv = d_raw[b][:].rearrange("b (p t s) -> b t s p", t=4, s=NP)
+        def x_transpose(n):
+            b, s = n // 6, n % 6
+            bank = ptr.tile([P, 4, P], F32, name="bank")
+            view = x_raw[b][:].bitcast(F32).rearrange("b (p t s) -> b t s p", t=4, s=NP)
             for t in range(4):
-                nc.tensor.transpose(d_bank[q][:, h, t, :], dv[:, t, s, :], ident[:])
-            return bank
+                nc.tensor.transpose(bank[:, t, :], view[:, t, s, :], ident[:])
+            x_bank[n] = bank
 
-        def slot_copy(bank, n, engine):
+        def x_copy(engine, n):
             q, h = n // 2, n % 2
-            if h == 0:
-                x_g[q] = work.tile([P, 2, 2, P, 4], BF16, name="xg", align_bytes=64)
-            copy(engine, x_g[q][:, h], bank[:].rearrange("p k t b -> p k b t"))
-
-        def dijet_copy(q):
-            d_g[q] = work.tile([P, 2, P, 4], BF16, name="dg", align_bytes=64)
-            nc.vector.tensor_tensor(
-                out=d_g[q][:], in0=d_bank[q][:].rearrange("p s t b -> p s b t"),
-                in1=sc[:].unsqueeze(1).unsqueeze(1).to_broadcast([P, 2, P, 4]), op=MULT)
+            if q not in x_g:
+                x_g[q] = work.tile([P, 2, 2, P, 4], BF16, name="xg", bufs=3, align_bytes=64)
+            copy(engine, x_g[q][:, :, h], x_bank[n][:].bitcast(BF16).rearrange("p t (b k) -> p k b t", k=2))
 
         def x_quant(q):
-            nc.vector.quantize_mx(out=x_c[q][:].rearrange("p s k b -> p (s k b)").bitcast(FP8X4),
-                                  scales=x_s[q][:].rearrange("p s k b -> p (s k b)"),
-                                  in_=x_g[q][:].rearrange("p s k b t -> p (s k b t)"))
+            nc.vector.quantize_mx(out=x_c[q][:].rearrange("p k h b -> p (k h b)").bitcast(FP8X4),
+                                  scales=x_s[q][:].rearrange("p k h b -> p (k h b)"),
+                                  in_=x_g[q][:].rearrange("p k h b t -> p (k h b t)"))
+
+        def d_widen(engine, b):
+            copy(engine, d_raw[b][:], d_byt[b][:].bitcast(FP8))
+
+        def d_shuffle(engine, b, t):
+            src = d_raw[b][:].bitcast(F32).rearrange("b (p t q) -> b t p q", t=4, q=3)
+            copy(engine, d_sh[b][:, :, t, :].rearrange("b q p -> b p q"), src[:, t])
+
+        def d_transpose(q):
+            bank = pdj.tile([P, 4, P], F32, name="dbank")
+            for t in range(4):
+                nc.tensor.transpose(bank[:, t, :], d_sh[q // 3][:, q % 3, t, :], ident[:])
+            d_bank[q] = bank
+
+        def d_scale(q):
+            d_g[q] = work.tile([P, 2, P, 4], BF16, name="dg", bufs=3, align_bytes=64)
+            nc.vector.tensor_tensor(
+                out=d_g[q][:], in0=d_bank[q][:].bitcast(BF16).rearrange("p t (b s) -> p s b t", s=2),
+                in1=sc[:].unsqueeze(1).unsqueeze(1).to_broadcast([P, 2, P, 4]), op=MULT)
 
         def d_quant(q):
-            nc.vector.quantize_mx(out=d_c[q][:].rearrange("p s b -> p (s b)").bitcast(FP8X4),
-                                  scales=d_s[q][:].rearrange("p s b -> p (s b)"),
+            nc.vector.quantize_mx(out=d_c[q][:].bitcast(FP8X4), scales=d_s[q][:],
                                   in_=d_g[q][:].rearrange("p s b t -> p (s b t)"))
 
-        def stage2(n):
-            q, h = n // 2, n % 2
-            acc = ps2.tile([P, 4, P], F32, name="acc2")
-            for o in range(4):
+        def stage2(q, a):
+            acc = ps2.tile([P, 2, 2 * P], F32, name="acc2")
+            for n in range(2):
                 for k in range(KW):
-                    g = POS[(o, k)]
-                    rhs = x_c[q][:, h, k, :] if k < 2 else d_c[q][:, h, :]
-                    rhs_s = x_s[q][:, h, k, :] if k < 2 else d_s[q][:, h, :]
-                    nc.tensor.matmul_mx(out=acc[:, o, :], lhsT=w2_c[:, g, :].bitcast(FP8X4), lhsT_scale=w2_s[:, g, :],
+                    g = POS[(2 * a + n, k)]
+                    rhs = x_c[q][:, k].rearrange("p h b -> p (h b)") if k < 2 else d_c[q][:]
+                    rhs_s = x_s[q][:, k].rearrange("p h b -> p (h b)") if k < 2 else d_s[q][:]
+                    nc.tensor.matmul_mx(out=acc[:, n, :], lhsT=w2_c[:, g, :].bitcast(FP8X4), lhsT_scale=w2_s[:, g, :],
                                         rhs=rhs.bitcast(FP8X4), rhs_scale=rhs_s, start=(k == 0), stop=(k == 2))
-            return acc
+            acc2[q, a] = acc
 
-        def h_copy(acc, n):
-            q, h = n // 2, n % 2
-            if h == 0:
-                h_g[q] = work.tile([P, 2, P, 4], BF16, name="hg", align_bytes=64)
-            nc.vector.tensor_tensor(out=h_g[q][:, h], in0=acc[:].rearrange("p t b -> p b t"),
-                                    in1=b2t[:].unsqueeze(1).to_broadcast([P, P, 4]), op=ADD)
+        def h_relu(q, t):
+            if q not in h_p:
+                h_p[q] = work.tile([P, 4, 2 * P], BF16, name="hp", bufs=3)
+            nc.scalar.activation(out=h_p[q][:, t, :], in_=acc2[q, t // 2][:, t % 2, :], func=RELU, bias=b2t[:, t : t + 1])
 
-        def h_relu(q):
-            nc.vector.tensor_scalar_max(out=h_g[q][:], in0=h_g[q][:], scalar1=0.0)
+        def h_interleave(q):
+            h_g[q] = work.tile([P, 2 * P, 4], BF16, name="hg", bufs=3, align_bytes=64)
+            nc.vector.tensor_copy(out=h_g[q][:].rearrange("p (c i) t -> p c t i", i=4),
+                                  in_=h_p[q][:].rearrange("p t (c i) -> p c t i", i=4))
 
         def h_quant(q):
-            nc.vector.quantize_mx(out=h_c[q][:].rearrange("p s b -> p (s b)").bitcast(FP8X4),
-                                  scales=h_s[q][:].rearrange("p s b -> p (s b)"),
-                                  in_=h_g[q][:].rearrange("p s b t -> p (s b t)"))
+            nc.vector.quantize_mx(out=h_c[q][:].bitcast(FP8X4), scales=h_s[q][:],
+                                  in_=h_g[q][:].rearrange("p n t -> p (n t)"))
 
-        def stage3(b, half, g):
+        def stage3(n):
+            b, half, g = n // 6, (n % 6) // 3, n % 3
+            q = b * 3 + g
             acc = ps3.tile([P, 2, 256], F32, name="acc3")
             o = slice(half * 256, half * 256 + 256)
-            q = b * 3 + g
             for h in range(2):
                 for k in range(KW):
-                    lhs = x_c[q][:, h, k, :] if k < 2 else h_c[q][:, h, :]
-                    lhs_s = x_s[q][:, h, k, :] if k < 2 else h_s[q][:, h, :]
+                    lhs = x_c[q][:, k, h, :] if k < 2 else h_c[q][:, h * P : (h + 1) * P]
+                    lhs_s = x_s[q][:, k, h, :] if k < 2 else h_s[q][:, h * P : (h + 1) * P]
                     nc.tensor.matmul_mx(out=acc[:, h, :], lhsT=lhs.bitcast(FP8X4), lhsT_scale=lhs_s,
                                         rhs=w3_c[:, k, o].bitcast(FP8X4), rhs_scale=w3_s[:, k, o],
                                         start=(k == 0), stop=(k == 2))
-            return acc
+            acc3[n] = acc
 
-        sums = {}
-
-        def add_res(acc, b, half, g):
-            if g == 0:
+        def add_residual(n):
+            b, half, g = n // 6, (n % 6) // 3, n % 3
+            if (b, half) not in sums:
                 sums[b, half] = work.tile([P, 3, 256, 2], F32, name="sums")
-            nc.vector.tensor_tensor(
-                out=sums[b, half][:, g], in0=acc[:].rearrange("p s o -> p o s"),
-                in1=res[b][:, half * 256 : half * 256 + 256, 2 * g : 2 * g + 2], op=ADD)
+            nc.vector.tensor_tensor(out=sums[b, half][:, g], in0=acc3[n][:].rearrange("p s o -> p o s"),
+                                    in1=res[b][:, g, half * 256 : half * 256 + 256, :], op=ADD)
 
-        def finish(b, half, o0, o1, engine):
-            fin = work.tile([P, o1 - o0, NP], F32, name="fin%d" % (o1 - o0))
+        def finish(engine, b, half, o0, o1):
+            fin = work.tile([P, o1 - o0, NP], F32, name="fin%d_%d_%d" % (b, half, o0), tag="fin", bufs=3)
             dst = fin[:].rearrange("p o (g s) -> p o g s", s=2)
             src = sums[b, half][:, :, o0:o1, :].rearrange("p g o s -> p o g s")
             if engine == "S":
@@ -227,57 +257,16 @@ def tile_dijetresnetblock_pa_kernel(tc, x, d_h1_bytes, d_h1_scale, d1, W2, b2, W
                 nc.vector.tensor_scalar_max(out=dst, in0=src, scalar1=0.0)
             nc.sync.dma_start(out=out[rows[b], half * 256 + o0 : half * 256 + o1, :], in_=fin[:])
 
-        later = {}
-
-        def at(step, fn, *args):
-            later.setdefault(step, []).append((fn, args))
-
-        plan = [("W2", j) for j in range(6)]
-        plan += [("X", 0), ("X", 1), ("W3", 0), ("X", 2), ("W3", 1), ("X", 3), ("S2", 0), ("W3", 2), ("X", 4),
-                 ("S2", 1), ("W3", 3), ("X", 5), ("S2", 2), ("W3", 4), ("X", 6), ("S2", 3), ("W3", 5), ("X", 7),
-                 ("S2", 4), ("U", 0), ("X", 8), ("S2", 5), ("U", 1), ("X", 9), ("S2", 6), ("U", 2), ("X", 10),
-                 ("S2", 7), ("U", 3), ("X", 11), ("S2", 8), ("U", 4), ("S2", 9), ("U", 5), ("S2", 10), ("S2", 11)]
-        plan += [("U", j) for j in range(6, 12)]
-
-        for step, (kind, n) in enumerate(plan):
-            if kind == "W2":
-                bank = weight_transposes(w2_raw, n)
-                w2_copy(bank, n, "V" if n in (1, 4) else "S")
-                at(step + 1, w2_quant, n)
-            elif kind == "X":
-                if n == 0:
-                    nc.vector.tensor_copy(out=d_raw[0][:], in_=d_byt[0][:].bitcast(FP8))
-                if n == 4:
-                    nc.scalar.copy(out=d_raw[1][:], in_=d_byt[1][:].bitcast(FP8))
-                bank = slot_transposes(n)
-                slot_copy(bank, n, "S")
-                if n % 2 == 1:
-                    dijet_copy(n // 2)
-                    at(step + 1, x_quant, n // 2)
-                    at(step + 1, d_quant, n // 2)
-            elif kind == "W3":
-                bank = weight_transposes(w3_raw, n)
-                w3_copy(bank, n, "S")
-                if n % 3 == 2:
-                    for k in range(KW):
-                        at(step + 1, w3_quant, k, n // 3)
-            elif kind == "S2":
-                acc = stage2(n)
-                h_copy(acc, n)
-                if n % 2 == 1:
-                    at(step + 1, h_relu, n // 2)
-                    at(step + 2 if n < 11 else step + 1, h_quant, n // 2)
-            else:
-                b, half, g = n // 6, (n % 6) // 3, n % 3
-                acc = stage3(b, half, g)
-                add_res(acc, b, half, g)
-                if g == 2:
-                    if (b, half) == (1, 1):
-                        at(step + 1, finish, b, half, 0, 128, "S")
-                        at(step + 1, finish, b, half, 128, 256, "V")
-                    else:
-                        at(step + 1, finish, b, half, 0, 256, "S")
-            for fn, args in later.pop(step, []):
-                fn(*args)
-        for fn, args in later.pop(len(plan), []):
-            fn(*args)
+        table = {
+            "ws": lambda e, i, o, u: w_shuffle(e, i, o, u), "wt": lambda e, i, j: w_transpose(i, j),
+            "wc": lambda e, i, j: w_copy(e, i, j), "w2q": lambda e, j: w2_quant(j), "w3q": lambda e, h, k: w3_quant(h, k),
+            "xt": lambda e, n: x_transpose(n), "xc": lambda e, n: x_copy(e, n), "xq": lambda e, q: x_quant(q),
+            "wid": lambda e, b: d_widen(e, b), "ds": lambda e, b, t: d_shuffle(e, b, t), "dt": lambda e, q: d_transpose(q),
+            "dc": lambda e, q: d_scale(q), "dq": lambda e, q: d_quant(q), "S2": lambda e, q, a: stage2(q, a),
+            "E": lambda e, q, t: h_relu(q, t), "hi": lambda e, q: h_interleave(q), "hq": lambda e, q: h_quant(q),
+            "U": lambda e, n: stage3(n), "F": lambda e, n: add_residual(n), "r": lambda e, b, g: residual(e, b, g),
+            "R": lambda e, b, h, o0, o1: finish(e, b, h, o0, o1),
+        }
+        for word in SEQ.split():
+            parts = word.split(":")
+            table[parts[0]](parts[1], *[int(v) for v in parts[2].split(",")])

@@ -21,21 +21,21 @@ GROUPS = [(0, 0), (0, 1), (0, 2), (1, 2), (1, 0), (1, 1), (2, 0), (2, 1), (2, 2)
 POS = {g: n for n, g in enumerate(GROUPS)}
 
 SEQ = """
-ws:V:0,0,0 ws:V:0,0,1 ws:V:0,1,0 wt:T:0,0 ws:V:0,2,0 wc:S:0,0 ws:V:0,1,1 ws:V:0,2,1 wt:T:0,1 ws:V:0,3,0
-wc:S:0,1 ws:V:0,3,1 w2q:V:0 wt:T:0,5 wt:T:0,3 wc:S:0,5 wt:T:0,4 wc:S:0,4 xt:T:0 wc:S:0,3 wid:V:0 xt:T:1 xc:S:0
-xt:T:5 xc:S:1 ws:V:1,0,1 ds:V:0,2 wt:T:0,2 ds:V:0,3 xc:S:5 w2q:V:2 xt:T:4 ds:V:0,1 ws:V:1,1,1 wc:S:0,2 xt:T:3
-xq:V:0 xc:S:4 ds:V:0,0 ws:V:1,0,0 dt:T:0 ws:V:1,1,0 xc:S:3 dc:V:0 wt:T:1,1 wt:T:1,0 wc:S:1,1 wt:T:1,2
-ws:V:1,3,0 wc:S:1,0 xt:T:2 dq:V:0 w2q:V:1 dt:T:1 ws:V:1,3,1 xc:S:2 ws:V:1,2,0 xt:T:6 dc:V:1 wc:S:1,2 S2:T:0,1
-ws:V:1,2,1 xc:S:6 r:G:1,0 dq:V:1 S2:T:0,0 xq:V:1 E:S:0,2 dt:T:2 E:S:0,0 wt:T:1,4 dc:V:2 wt:T:1,5 E:S:0,1
-wt:T:1,3 wc:S:1,4 S2:T:1,1 E:S:0,3 w3q:V:0,1 r:G:0,0 wc:S:1,3 w3q:V:0,0 S2:T:1,0 hi:V:0 E:S:1,2 wc:S:1,5
-xt:T:7 E:S:1,0 w3q:V:1,2 E:S:1,3 w3q:V:0,2 xt:T:8 E:S:1,1 w3q:V:1,1 wid:S:1 w3q:V:1,0 hq:V:0 r:G:0,1 xt:T:9
-hi:V:1 dq:V:2 xq:V:2 U:T:0 U:T:3 F:V:0 xc:S:7 S2:T:2,1 ds:V:1,2 r:G:0,2 ds:V:1,3 ds:V:1,0 S2:T:2,0 xc:S:9
-ds:V:1,1 hq:V:1 xq:V:3 dt:T:3 E:S:2,2 xt:T:10 E:S:2,0 dc:V:3 E:S:2,3 E:S:2,1 xt:T:11 r:G:1,2 F:V:3 dq:V:3
-dt:T:4 hi:V:2 xc:S:11 U:T:4 dc:V:4 S2:T:3,0 xc:S:8 hq:V:2 S2:T:3,1 dq:V:4 r:G:1,1 E:S:3,0 xq:V:4 dt:T:5
-E:S:3,2 U:T:2 E:S:3,1 dc:V:5 E:S:3,3 xc:S:10 S2:T:4,0 F:V:4 S2:T:4,1 dq:V:5 F:V:2 U:T:1 E:S:4,2 xq:V:5 E:S:4,0
-U:T:5 E:S:4,3 F:V:1 E:S:4,1 S2:T:5,1 hi:V:3 R:S:0,0,0,256 F:V:5 S2:T:5,0 hq:V:3 hi:V:4 U:T:6 E:S:5,2 E:S:5,0
-E:S:5,3 hq:V:4 E:S:5,1 F:V:6 U:T:7 R:S:0,1,0,256 hi:V:5 U:T:10 F:V:7 hq:V:5 U:T:9 F:V:10 U:T:11 F:V:9 U:T:8
-F:V:11 R:S:1,1,0,100 F:V:8 R:V:1,1,100,256 R:S:1,0,0,100 R:V:1,0,100,256
+ws:S:0,0,0 ws:V:0,0,1 ws:V:0,1,0 wt:T:0,0 ws:V:0,1,1 ws:S:0,2,0 ws:V:0,2,1 wt:T:0,1 ws:V:0,3,1 wt:T:0,2
+wc:S:0,0 ws:V:0,3,0 wc:S:0,1 wt:T:0,3 wc:V:0,2 wt:T:0,5 w2q:V:0 wc:S:0,3 wt:T:0,4 wc:V:0,5 wc:S:0,4 w2q:V:1
+xt:T:1 w2q:V:2 wid:V:0 xt:T:0 xc:S:1 xt:T:4 xc:S:0 ws:V:1,0,1 ds:V:0,0 xt:T:5 ds:V:0,1 ds:S:0,2 ds:V:0,3
+xq:V:0 xc:S:4 dt:T:0 ws:V:1,1,1 xt:T:3 ws:V:1,2,1 xc:S:5 dc:V:0 xt:T:2 ws:S:1,3,0 ws:V:1,3,1 dt:T:1 dq:V:0
+xc:S:2 wid:V:1 S2:T:0,1 ws:S:1,2,0 dc:V:1 wt:T:1,5 xc:S:3 wt:T:1,3 ds:V:1,3 r:V:0,2 E:S:0,2 xt:T:7 ds:S:1,1
+E:S:0,3 ds:V:1,2 wc:S:1,5 S2:T:0,0 ws:V:1,1,0 wc:S:1,3 xq:V:2 dt:T:2 E:S:0,0 wt:T:1,4 ds:V:1,0 xc:S:7 xq:V:1
+xt:T:6 dq:V:1 ws:V:1,0,0 E:S:0,1 xt:T:8 xc:S:6 dc:V:2 S2:T:1,0 wc:S:1,4 r:V:0,1 xc:S:8 S2:T:1,1 dq:V:2 r:V:1,2
+wt:T:1,2 E:S:1,0 dt:T:3 E:S:1,2 wt:T:1,0 E:S:1,1 xt:T:9 w3q:V:1,2 E:S:1,3 dc:V:3 wc:S:1,2 S2:T:2,0 hi:S:0
+w3q:V:1,0 xq:V:3 S2:T:2,1 xc:S:9 dq:V:3 r:V:0,0 xt:T:10 E:S:2,0 E:S:2,2 wt:T:1,1 hq:V:0 E:S:2,1 dt:T:4 xq:V:4
+wc:S:1,0 S2:T:3,1 dc:V:4 wc:S:1,1 xt:T:11 E:S:2,3 w3q:V:1,1 E:S:3,2 hi:V:1 hi:S:2 dt:T:5 w3q:V:0,0 S2:T:3,0
+w3q:V:0,2 E:S:3,3 dq:V:4 U:T:3 hq:V:1 E:S:3,0 hq:V:2 xc:S:11 dc:V:5 S2:T:4,1 U:T:5 E:S:3,1 F:V:3 xc:S:10
+dq:V:5 S2:T:4,0 w3q:V:0,1 F:V:5 E:S:4,2 U:T:4 E:S:4,0 xq:V:5 E:S:4,3 hi:S:3 r:V:1,1 S2:T:5,0 U:T:2 F:V:4
+E:S:4,1 E:S:5,0 hq:V:3 S2:T:5,1 hi:S:4 F:V:2 U:T:0 r:V:1,0 E:S:5,2 U:T:1 E:S:5,1 F:V:0 E:S:5,3 R:S:0,1,0,256
+hq:V:4 U:T:6 F:V:1 hi:V:5 U:T:7 R:S:0,0,0,256 F:V:6 hq:V:5 U:T:9 F:V:7 U:T:11 F:V:9 U:T:10 F:V:11 U:T:8 F:V:10
+R:S:1,1,0,100 F:V:8 R:V:1,1,100,256 R:S:1,0,0,100 R:V:1,0,100,256
 """
 
 
@@ -59,6 +59,7 @@ def tile_dijetresnetblock_pa_kernel(tc, x, d_h1_bytes, d_h1_scale, d1, W2, b2, W
         res = [keep.tile([P, 3, ND, 2], F32, name="res%d" % b) for b in range(2)]
         sc = keep.tile([P, 4], F32, name="sc")
         b2t = keep.tile([P, 4], BF16, name="b2t")
+        b2f = keep.tile([P, 4], F32, name="b2f")
         b3t = keep.tile([P, ND], BF16, name="b3t")
         rows = [slice(b * P, (b + 1) * P) for b in range(2)]
 
@@ -90,6 +91,8 @@ def tile_dijetresnetblock_pa_kernel(tc, x, d_h1_bytes, d_h1_scale, d1, W2, b2, W
         warm = keep.tile([P, 1], F32, name="warm")
         nc.vector.memset(warm[:], 0.0)
         nc.scalar.activation(out=warm[:], in_=warm[:], func=RELU)
+
+        nc.gpsimd.tensor_copy(out=b2f[:], in_=b2t[:])
 
         def copy(engine, out_ap, in_ap):
             if engine == "S":
@@ -212,15 +215,18 @@ def tile_dijetresnetblock_pa_kernel(tc, x, d_h1_bytes, d_h1_scale, d1, W2, b2, W
                                         rhs=rhs.bitcast(FP8X4), rhs_scale=rhs_s, start=(k == 0), stop=(k == 2))
             acc2[q, a] = acc
 
-        def h_relu(q, t):
+        def h_relu(engine, q, t):
             if q not in h_p:
                 h_p[q] = work.tile([P, 4, 2 * P], BF16, name="hp", bufs=3)
-            nc.scalar.activation(out=h_p[q][:, t, :], in_=acc2[q, t // 2][:, t % 2, :], func=RELU, bias=b2t[:, t : t + 1])
+            if engine == "S":
+                nc.scalar.activation(out=h_p[q][:, t, :], in_=acc2[q, t // 2][:, t % 2, :], func=RELU, bias=b2f[:, t : t + 1])
+            else:
+                nc.vector.tensor_scalar(out=h_p[q][:, t, :], in0=acc2[q, t // 2][:, t % 2, :], scalar1=b2f[:, t : t + 1],
+                                        scalar2=0.0, op0=ADD, op1=mybir.AluOpType.max)
 
-        def h_interleave(q):
+        def h_interleave(engine, q):
             h_g[q] = work.tile([P, 2 * P, 4], BF16, name="hg", bufs=3, align_bytes=64)
-            nc.vector.tensor_copy(out=h_g[q][:].rearrange("p (c i) t -> p c t i", i=4),
-                                  in_=h_p[q][:].rearrange("p t (c i) -> p c t i", i=4))
+            copy(engine, h_g[q][:].rearrange("p (c i) t -> p c t i", i=4), h_p[q][:].rearrange("p t (c i) -> p c t i", i=4))
 
         def h_quant(q):
             nc.vector.quantize_mx(out=h_c[q][:].bitcast(FP8X4), scales=h_s[q][:],
@@ -263,7 +269,7 @@ def tile_dijetresnetblock_pa_kernel(tc, x, d_h1_bytes, d_h1_scale, d1, W2, b2, W
             "xt": lambda e, n: x_transpose(n), "xc": lambda e, n: x_copy(e, n), "xq": lambda e, q: x_quant(q),
             "wid": lambda e, b: d_widen(e, b), "ds": lambda e, b, t: d_shuffle(e, b, t), "dt": lambda e, q: d_transpose(q),
             "dc": lambda e, q: d_scale(q), "dq": lambda e, q: d_quant(q), "S2": lambda e, q, a: stage2(q, a),
-            "E": lambda e, q, t: h_relu(q, t), "hi": lambda e, q: h_interleave(q), "hq": lambda e, q: h_quant(q),
+            "E": lambda e, q, t: h_relu(e, q, t), "hi": lambda e, q: h_interleave(e, q), "hq": lambda e, q: h_quant(q),
             "U": lambda e, n: stage3(n), "F": lambda e, n: add_residual(n), "r": lambda e, b, g: residual(e, b, g),
             "R": lambda e, b, h, o0, o1: finish(e, b, h, o0, o1),
         }

@@ -20,22 +20,20 @@ FLOPS = 2 * 2 * N * NP * KW * ND * ND
 GROUPS = [(0, 0), (0, 1), (0, 2), (1, 2), (1, 0), (1, 1), (2, 0), (2, 1), (2, 2), (3, 2), (3, 0), (3, 1)]
 POS = {g: n for n, g in enumerate(GROUPS)}
 
+GROUP_SIZES = [2, 4, 2, 4]
 SEQ = """
-ws:S:0,0,0 ws:V:0,0,1 ws:V:0,1,0 wt:T:0,0 ws:V:0,1,1 ws:S:0,2,0 ws:V:0,2,1 wt:T:0,1 ws:V:0,3,1 wt:T:0,2
-wc:S:0,0 ws:V:0,3,0 wc:S:0,1 wt:T:0,3 wc:V:0,2 wt:T:0,5 w2q:V:0 wc:S:0,3 wt:T:0,4 wc:V:0,5 wc:S:0,4 w2q:V:1
-xt:T:1 w2q:V:2 wid:V:0 xt:T:0 xc:S:1 xt:T:4 xc:S:0 ws:V:1,0,1 ds:V:0,0 xt:T:5 ds:V:0,1 ds:S:0,2 ds:V:0,3
-xq:V:0 xc:S:4 dt:T:0 ws:V:1,1,1 xt:T:3 ws:V:1,2,1 xc:S:5 dc:V:0 xt:T:2 ws:S:1,3,0 ws:V:1,3,1 dt:T:1 dq:V:0
-xc:S:2 wid:V:1 S2:T:0,1 ws:S:1,2,0 dc:V:1 wt:T:1,5 xc:S:3 wt:T:1,3 ds:V:1,3 r:V:0,2 E:S:0,2 xt:T:7 ds:S:1,1
-E:S:0,3 ds:V:1,2 wc:S:1,5 S2:T:0,0 ws:V:1,1,0 wc:S:1,3 xq:V:2 dt:T:2 E:S:0,0 wt:T:1,4 ds:V:1,0 xc:S:7 xq:V:1
-xt:T:6 dq:V:1 ws:V:1,0,0 E:S:0,1 xt:T:8 xc:S:6 dc:V:2 S2:T:1,0 wc:S:1,4 r:V:0,1 xc:S:8 S2:T:1,1 dq:V:2 r:V:1,2
-wt:T:1,2 E:S:1,0 dt:T:3 E:S:1,2 wt:T:1,0 E:S:1,1 xt:T:9 w3q:V:1,2 E:S:1,3 dc:V:3 wc:S:1,2 S2:T:2,0 hi:S:0
-w3q:V:1,0 xq:V:3 S2:T:2,1 xc:S:9 dq:V:3 r:V:0,0 xt:T:10 E:S:2,0 E:S:2,2 wt:T:1,1 hq:V:0 E:S:2,1 dt:T:4 xq:V:4
-wc:S:1,0 S2:T:3,1 dc:V:4 wc:S:1,1 xt:T:11 E:S:2,3 w3q:V:1,1 E:S:3,2 hi:V:1 hi:S:2 dt:T:5 w3q:V:0,0 S2:T:3,0
-w3q:V:0,2 E:S:3,3 dq:V:4 U:T:3 hq:V:1 E:S:3,0 hq:V:2 xc:S:11 dc:V:5 S2:T:4,1 U:T:5 E:S:3,1 F:V:3 xc:S:10
-dq:V:5 S2:T:4,0 w3q:V:0,1 F:V:5 E:S:4,2 U:T:4 E:S:4,0 xq:V:5 E:S:4,3 hi:S:3 r:V:1,1 S2:T:5,0 U:T:2 F:V:4
-E:S:4,1 E:S:5,0 hq:V:3 S2:T:5,1 hi:S:4 F:V:2 U:T:0 r:V:1,0 E:S:5,2 U:T:1 E:S:5,1 F:V:0 E:S:5,3 R:S:0,1,0,256
-hq:V:4 U:T:6 F:V:1 hi:V:5 U:T:7 R:S:0,0,0,256 F:V:6 hq:V:5 U:T:9 F:V:7 U:T:11 F:V:9 U:T:10 F:V:11 U:T:8 F:V:10
-R:S:1,1,0,100 F:V:8 R:V:1,1,100,256 R:S:1,0,0,100 R:V:1,0,100,256
+ws:V:0,0,0,64 ws:S:0,0,64,128 wid:V:0 wt:T:0,0 ws:S:0,1,0,128 bb:T:0 ws:V:0,2,0,128 ds:V:0 bc:S:0 wt:T:0,2 wc:S:0,0
+wt:T:0,1 ws:V:0,3,0,128 dt:T:2 wc:S:0,2 wt:T:0,3 dc:V:2 wc:S:0,1 wt:T:0,5 wc:S:0,3 wt:T:0,4 w2q:V:0 dt:T:1 wc:S:0,5
+w2q:V:1 xt:T:0 wc:S:0,4 dc:V:1 ws:S:1,0,0,128 xt:T:5 ws:V:1,1,0,128 dt:T:0 xt:T:4 xc:S:5 ws:V:1,3,0,128 ws:V:1,2,0,128
+xc:S:0 xt:T:1 dc:V:0 xc:S:4 wt:T:1,4 dq:V:1 xt:T:3 wc:S:1,4 wid:V:1 xc:S:1 xt:T:2 xc:S:3 wt:T:1,3 r:V:0,1 wt:T:1,5
+wc:S:1,3 xt:T:11 xc:S:2 xq:V:0 xt:T:8 w2q:V:2 wc:S:1,5 xt:T:9 xq:V:1 ds:S:1 xt:T:10 dq:V:0 xc:V:8 xc:S:9 S2:T:1,0
+r:V:0,0 xc:S:11 dt:T:5 S2:T:0,0 dc:V:5 xc:S:10 dt:T:3 wt:T:1,0 r:V:1,1 E:S:1,0 dt:T:4 wt:T:1,1 E:S:0,1 S2:T:0,1
+E:S:0,0 wc:S:1,0 dc:V:4 S2:T:1,1 E:S:0,2 E:S:0,3 wt:T:1,2 dc:V:3 wc:S:1,1 xt:T:7 E:S:1,1 xq:V:3 S2:T:1,3 wc:S:1,2
+hi:S:0 S2:T:1,2 w3q:V:2 xt:T:6 dq:V:3 E:S:1,3 w3q:V:1 E:S:1,2 S2:T:3,3 w3q:V:0 xc:S:6 hq:V:0 S2:T:3,1 dq:V:2 hi:V:1
+E:S:3,3 U:T:0 E:S:3,1 S2:T:3,0 xc:S:7 F:V:0 S2:T:3,2 hq:V:1 U:T:3 E:S:3,0 xq:V:2 E:S:3,2 U:T:5 F:V:3 S2:T:2,0 hi:S:3
+r:V:1,0 U:T:4 S2:T:2,1 F:V:5 F:V:4 U:T:1 E:S:2,1 E:S:2,2 hq:V:3 U:T:2 E:S:2,3 F:V:1 E:S:2,0 R:S:0,1,0,256 U:T:10
+hi:V:2 F:V:2 hq:V:2 U:T:11 R:S:0,0,0,256 F:V:10 U:T:9 F:V:11 U:T:7 F:V:9 U:T:8 F:V:7 R:S:1,1,0,100 R:V:1,1,100,256
+U:T:6 F:V:8 F:V:6 R:S:1,0,0,100 R:V:1,0,100,256
 """
 
 
@@ -44,8 +42,7 @@ def tile_dijetresnetblock_pa_kernel(tc, x, d_h1_bytes, d_h1_scale, d1, W2, b2, W
     with ExitStack() as ctx:
         keep = ctx.enter_context(tc.tile_pool(name="keep", bufs=1))
         work = ctx.enter_context(tc.tile_pool(name="work", bufs=2))
-        ptr = ctx.enter_context(tc.psum_pool(name="ptr", bufs=3))
-        pdj = ctx.enter_context(tc.psum_pool(name="pdj", bufs=1))
+        ptr = ctx.enter_context(tc.psum_pool(name="ptr", bufs=4))
         ps2 = ctx.enter_context(tc.psum_pool(name="ps2", bufs=2))
         ps3 = ctx.enter_context(tc.psum_pool(name="ps3", bufs=2))
         ctx.enter_context(tc.manual_schedule())
@@ -56,11 +53,13 @@ def tile_dijetresnetblock_pa_kernel(tc, x, d_h1_bytes, d_h1_scale, d1, W2, b2, W
         d_byt = [keep.tile([P, ND * NP], U8, name="d_byt%d" % b) for b in range(2)]
         d_raw = [keep.tile([P, ND * NP], BF16, name="d_raw%d" % b, tag="d_raw") for b in range(2)]
         d1_raw = [keep.tile([P, ND, NP], BF16, name="d1_raw%d" % b, tag="raw0_%d" % b) for b in range(2)]
-        res = [keep.tile([P, 3, ND, 2], F32, name="res%d" % b) for b in range(2)]
+        res = [[keep.tile([P, 3, 256, 2], F32, name="res%d_%d" % (b, h), tag="res%d" % h if b == 0 else "raw1_%d" % h) for h in range(2)] for b in range(2)]
         sc = keep.tile([P, 4], F32, name="sc")
         b2t = keep.tile([P, 4], BF16, name="b2t")
         b2f = keep.tile([P, 4], F32, name="b2f")
-        b3t = keep.tile([P, ND], BF16, name="b3t")
+        b3_row = keep.tile([P, ND], BF16, name="b3_row")
+        b3t = keep.tile([P, ND], F32, name="b3t")
+        ones = keep.tile([P, P], BF16, name="ones")
         rows = [slice(b * P, (b + 1) * P) for b in range(2)]
 
         def load_w(i, t):
@@ -72,16 +71,24 @@ def tile_dijetresnetblock_pa_kernel(tc, x, d_h1_bytes, d_h1_scale, d1, W2, b2, W
         def load_d(b):
             nc.sync.dma_start(out=d_byt[b][:], in_=d_h1_bytes[rows[b]].rearrange("b i s -> b (i s)"))
 
-        for t in range(4):
+        def load_small():
+            nc.sync.dma_start(out=sc[:], in_=d_h1_scale.rearrange("o (p t) w -> p (o t w)", t=4))
+            nc.sync.dma_start(out=b3_row[0:1, :], in_=b3.unsqueeze(0))
+
+        nc.vector.memset(b3_row[:], 0.0)
+        nc.vector.memset(ones[:], 1.0)
+        for c in range(2):
+            cols = slice(c * ND * KW // 2, (c + 1) * ND * KW // 2)
+            nc.sync.dma_start(out=w_raw[0][0][:, 0, cols], in_=w_src[0][:, 0, cols])
+        load_d(0)
+        load_small()
+        for t in range(1, 4):
             load_w(0, t)
         load_x(0)
-        load_d(0)
-        nc.sync.dma_start(out=sc[:], in_=d_h1_scale.rearrange("o (p t) w -> p (o t w)", t=4))
         nc.sync.dma_start(out=b2t[:], in_=b2.rearrange("(p t) -> p t", t=4))
         for t in range(4):
             load_w(1, t)
         load_d(1)
-        nc.sync.dma_start(out=b3t[:], in_=b3.partition_broadcast(P))
         nc.sync.dma_start(out=d1_raw[0][:], in_=d1[rows[0]])
         load_x(1)
         nc.sync.dma_start(out=d1_raw[1][:], in_=d1[rows[1]])
@@ -91,7 +98,6 @@ def tile_dijetresnetblock_pa_kernel(tc, x, d_h1_bytes, d_h1_scale, d1, W2, b2, W
         warm = keep.tile([P, 1], F32, name="warm")
         nc.vector.memset(warm[:], 0.0)
         nc.scalar.activation(out=warm[:], in_=warm[:], func=RELU)
-
         nc.gpsimd.tensor_copy(out=b2f[:], in_=b2t[:])
 
         def copy(engine, out_ap, in_ap):
@@ -100,27 +106,33 @@ def tile_dijetresnetblock_pa_kernel(tc, x, d_h1_bytes, d_h1_scale, d1, W2, b2, W
             else:
                 nc.vector.tensor_copy(out=out_ap, in_=in_ap)
 
-        OC = 64
+        def b3_spread():
+            bank = ptr.tile([P, ND], F32, name="bank")
+            nc.tensor.matmul(bank[:], lhsT=ones[:], rhs=b3_row[:], start=True, stop=True)
+            w_bank["b3"] = bank
 
-        def residual(engine, b, g):
-            for o in range(0, ND, OC if engine == "G" else ND):
-                c = slice(o, o + (OC if engine == "G" else ND))
-                eng = nc.gpsimd if engine == "G" else nc.vector
-                eng.tensor_tensor(out=res[b][:, g, c, :], in0=d1_raw[b][:, c, 2 * g : 2 * g + 2],
-                                  in1=b3t[:, c].unsqueeze(2).to_broadcast([P, c.stop - c.start, 2]), op=ADD)
+        def residual(b, half):
+            o = slice(half * 256, half * 256 + 256)
+            nc.vector.tensor_tensor(out=res[b][half][:], in0=d1_raw[b][:, o, :].rearrange("b o (g s) -> b g o s", s=2),
+                                    in1=b3t[:, o].unsqueeze(1).unsqueeze(3).to_broadcast([P, 3, 256, 2]), op=ADD)
 
         w_sh = [[keep.tile([P, KW, 2, P, 2], BF16, name="w_sh%d_%d" % (i, o), tag="w_sh%d" % o) for o in range(4)] for i in range(2)]
-        w2_g = keep.tile([P, 12, P, 2], F32, name="w2_g", tag="w_g", align_bytes=64)
+        w2_g = keep.tile([P, 12, P, 2], F32, name="w2_g", align_bytes=64)
         w2_c = keep.tile([P, 12, P], U32, name="w2_c", align_bytes=64)
         w2_s = keep.tile([P, 12, P], U8, name="w2_s", align_bytes=64)
-        w3_g = keep.tile([P, KW, ND, 2], F32, name="w3_g", tag="w_g", align_bytes=64)
+        w3_g = keep.tile([P, KW, ND, 2], F32, name="w3_g", align_bytes=64)
         w3_c = keep.tile([P, KW, ND], U32, name="w3_c", align_bytes=64)
         w3_s = keep.tile([P, KW, ND], U8, name="w3_s", align_bytes=64)
         w_bank = {}
 
-        def w_shuffle(engine, i, o, u):
-            src = w_raw[i][o // 2][:, o % 2, :].rearrange("m (p u e k) -> m u p k e", u=2, e=2, k=KW)
-            copy(engine, w_sh[i][o][:, :, u, :, :].rearrange("m k p e -> m p k e"), src[:, u])
+        def w_shuffle(engine, i, o, p0, p1):
+            src = w_raw[i][o // 2][:, o % 2, :].rearrange("m (p u e k) -> m u p k e", u=2, e=2, k=KW)[:, :, p0:p1]
+            dst = w_sh[i][o][:].rearrange("m k u p e -> m u p k e")[:, :, p0:p1]
+            if engine == "V":
+                nc.vector.tensor_copy(out=dst, in_=src)
+            else:
+                for u in range(2):
+                    nc.scalar.copy(out=dst[:, u], in_=src[:, u])
 
         def w_transpose(i, j):
             bank = ptr.tile([P, 2, 2, P], F32, name="bank")
@@ -148,17 +160,21 @@ def tile_dijetresnetblock_pa_kernel(tc, x, d_h1_bytes, d_h1_scale, d1, W2, b2, W
                 scales=w2_s[:, g, :].rearrange("p n m -> p (n m)"),
                 in_=w2_g[:, g, :, :].rearrange("p n m u -> p (n m u)").bitcast(BF16))
 
-        def w3_quant(half, k):
-            g = slice(half * 256, half * 256 + 256)
-            nc.vector.quantize_mx(out=w3_c[:, k, g].bitcast(FP8X4), scales=w3_s[:, k, g],
-                                  in_=w3_g[:, k, g, :].rearrange("p m u -> p (m u)").bitcast(BF16))
+        def w3_quant(k):
+            nc.vector.quantize_mx(out=w3_c[:, k, :].bitcast(FP8X4), scales=w3_s[:, k, :],
+                                  in_=w3_g[:, k, :, :].rearrange("p m u -> p (m u)").bitcast(BF16))
 
-        x_c = [keep.tile([P, 2, 2, P], U32, name="x_c%d" % q, align_bytes=64) for q in range(6)]
-        x_s = [keep.tile([P, 2, 2, P], U8, name="x_s%d" % q, align_bytes=64) for q in range(6)]
-        d_c = [keep.tile([P, 2 * P], U32, name="d_c%d" % q, align_bytes=64) for q in range(6)]
-        d_s = [keep.tile([P, 2 * P], U8, name="d_s%d" % q, align_bytes=64) for q in range(6)]
-        h_c = [keep.tile([P, 2 * P], U32, name="h_c%d" % q, align_bytes=64) for q in range(6)]
-        h_s = [keep.tile([P, 2 * P], U8, name="h_s%d" % q, align_bytes=64) for q in range(6)]
+        starts = [sum(GROUP_SIZES[:q]) for q in range(len(GROUP_SIZES))]
+        group_of = {}
+        for q in range(len(GROUP_SIZES)):
+            for n in range(starts[q], starts[q] + GROUP_SIZES[q]):
+                group_of[n] = (q, n - starts[q])
+        x_c = [keep.tile([P, 2, z * P], U32, name="x_c%d" % q, align_bytes=64) for q, z in enumerate(GROUP_SIZES)]
+        x_s = [keep.tile([P, 2, z * P], U8, name="x_s%d" % q, align_bytes=64) for q, z in enumerate(GROUP_SIZES)]
+        d_c = [keep.tile([P, z * P], U32, name="d_c%d" % q, align_bytes=64) for q, z in enumerate(GROUP_SIZES)]
+        d_s = [keep.tile([P, z * P], U8, name="d_s%d" % q, align_bytes=64) for q, z in enumerate(GROUP_SIZES)]
+        h_c = [keep.tile([P, z * P], U32, name="h_c%d" % q, align_bytes=64) for q, z in enumerate(GROUP_SIZES)]
+        h_s = [keep.tile([P, z * P], U8, name="h_s%d" % q, align_bytes=64) for q, z in enumerate(GROUP_SIZES)]
         d_sh = [keep.tile([P, 3, 4, P], F32, name="d_sh%d" % b) for b in range(2)]
         x_bank, d_bank, x_g, d_g, acc2, h_p, h_g, acc3, sums = {}, {}, {}, {}, {}, {}, {}, {}, {}
 
@@ -171,77 +187,80 @@ def tile_dijetresnetblock_pa_kernel(tc, x, d_h1_bytes, d_h1_scale, d1, W2, b2, W
             x_bank[n] = bank
 
         def x_copy(engine, n):
-            q, h = n // 2, n % 2
+            q, r = group_of[n]
             if q not in x_g:
-                x_g[q] = work.tile([P, 2, 2, P, 4], BF16, name="xg", bufs=3, align_bytes=64)
-            copy(engine, x_g[q][:, :, h], x_bank[n][:].bitcast(BF16).rearrange("p t (b k) -> p k b t", k=2))
+                x_g[q] = work.tile([P, 2, GROUP_SIZES[q] * P, 4], BF16, name="xg", bufs=2, align_bytes=64)
+            copy(engine, x_g[q][:, :, r * P : (r + 1) * P, :], x_bank[n][:].bitcast(BF16).rearrange("p t (b k) -> p k b t", k=2))
 
         def x_quant(q):
-            nc.vector.quantize_mx(out=x_c[q][:].rearrange("p k h b -> p (k h b)").bitcast(FP8X4),
-                                  scales=x_s[q][:].rearrange("p k h b -> p (k h b)"),
-                                  in_=x_g[q][:].rearrange("p k h b t -> p (k h b t)"))
+            nc.vector.quantize_mx(out=x_c[q][:].rearrange("p k n -> p (k n)").bitcast(FP8X4),
+                                  scales=x_s[q][:].rearrange("p k n -> p (k n)"),
+                                  in_=x_g[q][:].rearrange("p k n t -> p (k n t)"))
 
         def d_widen(engine, b):
             copy(engine, d_raw[b][:], d_byt[b][:].bitcast(FP8))
 
-        def d_shuffle(engine, b, t):
-            src = d_raw[b][:].bitcast(F32).rearrange("b (p t q) -> b t p q", t=4, q=3)
-            copy(engine, d_sh[b][:, :, t, :].rearrange("b q p -> b p q"), src[:, t])
+        def d_shuffle(engine, b):
+            copy(engine, d_sh[b][:].rearrange("b q t p -> b t p q"), d_raw[b][:].bitcast(F32).rearrange("b (p t q) -> b t p q", t=4, q=3))
 
-        def d_transpose(q):
-            bank = pdj.tile([P, 4, P], F32, name="dbank")
+        def d_transpose(pair):
+            bank = ptr.tile([P, 4, P], F32, name="bank")
             for t in range(4):
-                nc.tensor.transpose(bank[:, t, :], d_sh[q // 3][:, q % 3, t, :], ident[:])
-            d_bank[q] = bank
+                nc.tensor.transpose(bank[:, t, :], d_sh[pair // 3][:, pair % 3, t, :], ident[:])
+            d_bank[pair] = bank
 
-        def d_scale(q):
-            d_g[q] = work.tile([P, 2, P, 4], BF16, name="dg", bufs=3, align_bytes=64)
+        def d_scale(pair):
+            q, r = group_of[2 * pair]
+            if q not in d_g:
+                d_g[q] = work.tile([P, GROUP_SIZES[q] * P, 4], BF16, name="dg", align_bytes=64)
             nc.vector.tensor_tensor(
-                out=d_g[q][:], in0=d_bank[q][:].bitcast(BF16).rearrange("p t (b s) -> p s b t", s=2),
+                out=d_g[q][:, r * P : (r + 2) * P, :].rearrange("p (s b) t -> p s b t", s=2),
+                in0=d_bank[pair][:].bitcast(BF16).rearrange("p t (b s) -> p s b t", s=2),
                 in1=sc[:].unsqueeze(1).unsqueeze(1).to_broadcast([P, 2, P, 4]), op=MULT)
 
         def d_quant(q):
-            nc.vector.quantize_mx(out=d_c[q][:].bitcast(FP8X4), scales=d_s[q][:],
-                                  in_=d_g[q][:].rearrange("p s b t -> p (s b t)"))
+            nc.vector.quantize_mx(out=d_c[q][:].bitcast(FP8X4), scales=d_s[q][:], in_=d_g[q][:].rearrange("p n t -> p (n t)"))
 
         def stage2(q, a):
-            acc = ps2.tile([P, 2, 2 * P], F32, name="acc2")
-            for n in range(2):
+            z = GROUP_SIZES[q]
+            per = 4 // z
+            acc = ps2.tile([P, per, z * P], F32, name="acc2")
+            for n in range(per):
                 for k in range(KW):
-                    g = POS[(2 * a + n, k)]
-                    rhs = x_c[q][:, k].rearrange("p h b -> p (h b)") if k < 2 else d_c[q][:]
-                    rhs_s = x_s[q][:, k].rearrange("p h b -> p (h b)") if k < 2 else d_s[q][:]
+                    g = POS[(per * a + n, k)]
+                    rhs = x_c[q][:, k] if k < 2 else d_c[q][:]
+                    rhs_s = x_s[q][:, k] if k < 2 else d_s[q][:]
                     nc.tensor.matmul_mx(out=acc[:, n, :], lhsT=w2_c[:, g, :].bitcast(FP8X4), lhsT_scale=w2_s[:, g, :],
                                         rhs=rhs.bitcast(FP8X4), rhs_scale=rhs_s, start=(k == 0), stop=(k == 2))
-            acc2[q, a] = acc
+                acc2[q, per * a + n] = acc[:, n, :]
 
         def h_relu(engine, q, t):
             if q not in h_p:
-                h_p[q] = work.tile([P, 4, 2 * P], BF16, name="hp", bufs=3)
+                h_p[q] = work.tile([P, 4, GROUP_SIZES[q] * P], BF16, name="hp")
             if engine == "S":
-                nc.scalar.activation(out=h_p[q][:, t, :], in_=acc2[q, t // 2][:, t % 2, :], func=RELU, bias=b2f[:, t : t + 1])
+                nc.scalar.activation(out=h_p[q][:, t, :], in_=acc2[q, t], func=RELU, bias=b2f[:, t : t + 1])
             else:
-                nc.vector.tensor_scalar(out=h_p[q][:, t, :], in0=acc2[q, t // 2][:, t % 2, :], scalar1=b2f[:, t : t + 1],
-                                        scalar2=0.0, op0=ADD, op1=mybir.AluOpType.max)
+                nc.vector.tensor_scalar(out=h_p[q][:, t, :], in0=acc2[q, t], scalar1=b2f[:, t : t + 1], scalar2=0.0,
+                                        op0=ADD, op1=mybir.AluOpType.max)
 
         def h_interleave(engine, q):
-            h_g[q] = work.tile([P, 2 * P, 4], BF16, name="hg", bufs=3, align_bytes=64)
+            h_g[q] = work.tile([P, GROUP_SIZES[q] * P, 4], BF16, name="hg", align_bytes=64)
             copy(engine, h_g[q][:].rearrange("p (c i) t -> p c t i", i=4), h_p[q][:].rearrange("p t (c i) -> p c t i", i=4))
 
         def h_quant(q):
-            nc.vector.quantize_mx(out=h_c[q][:].bitcast(FP8X4), scales=h_s[q][:],
-                                  in_=h_g[q][:].rearrange("p n t -> p (n t)"))
+            nc.vector.quantize_mx(out=h_c[q][:].bitcast(FP8X4), scales=h_s[q][:], in_=h_g[q][:].rearrange("p n t -> p (n t)"))
 
         def stage3(n):
             b, half, g = n // 6, (n % 6) // 3, n % 3
-            q = b * 3 + g
             acc = ps3.tile([P, 2, 256], F32, name="acc3")
             o = slice(half * 256, half * 256 + 256)
-            for h in range(2):
+            for s in range(2):
+                q, r = group_of[6 * b + 2 * g + s]
+                c = slice(r * P, (r + 1) * P)
                 for k in range(KW):
-                    lhs = x_c[q][:, k, h, :] if k < 2 else h_c[q][:, h * P : (h + 1) * P]
-                    lhs_s = x_s[q][:, k, h, :] if k < 2 else h_s[q][:, h * P : (h + 1) * P]
-                    nc.tensor.matmul_mx(out=acc[:, h, :], lhsT=lhs.bitcast(FP8X4), lhsT_scale=lhs_s,
+                    lhs = x_c[q][:, k, c] if k < 2 else h_c[q][:, c]
+                    lhs_s = x_s[q][:, k, c] if k < 2 else h_s[q][:, c]
+                    nc.tensor.matmul_mx(out=acc[:, s, :], lhsT=lhs.bitcast(FP8X4), lhsT_scale=lhs_s,
                                         rhs=w3_c[:, k, o].bitcast(FP8X4), rhs_scale=w3_s[:, k, o],
                                         start=(k == 0), stop=(k == 2))
             acc3[n] = acc
@@ -251,10 +270,10 @@ def tile_dijetresnetblock_pa_kernel(tc, x, d_h1_bytes, d_h1_scale, d1, W2, b2, W
             if (b, half) not in sums:
                 sums[b, half] = work.tile([P, 3, 256, 2], F32, name="sums")
             nc.vector.tensor_tensor(out=sums[b, half][:, g], in0=acc3[n][:].rearrange("p s o -> p o s"),
-                                    in1=res[b][:, g, half * 256 : half * 256 + 256, :], op=ADD)
+                                    in1=res[b][half][:, g], op=ADD)
 
         def finish(engine, b, half, o0, o1):
-            fin = work.tile([P, o1 - o0, NP], F32, name="fin%d_%d_%d" % (b, half, o0), tag="fin", bufs=3)
+            fin = work.tile([P, o1 - o0, NP], F32, name="fin%d_%d_%d" % (b, half, o0), tag="fin", bufs=2)
             dst = fin[:].rearrange("p o (g s) -> p o g s", s=2)
             src = sums[b, half][:, :, o0:o1, :].rearrange("p g o s -> p o g s")
             if engine == "S":
@@ -264,14 +283,14 @@ def tile_dijetresnetblock_pa_kernel(tc, x, d_h1_bytes, d_h1_scale, d1, W2, b2, W
             nc.sync.dma_start(out=out[rows[b], half * 256 + o0 : half * 256 + o1, :], in_=fin[:])
 
         table = {
-            "ws": lambda e, i, o, u: w_shuffle(e, i, o, u), "wt": lambda e, i, j: w_transpose(i, j),
-            "wc": lambda e, i, j: w_copy(e, i, j), "w2q": lambda e, j: w2_quant(j), "w3q": lambda e, h, k: w3_quant(h, k),
-            "xt": lambda e, n: x_transpose(n), "xc": lambda e, n: x_copy(e, n), "xq": lambda e, q: x_quant(q),
-            "wid": lambda e, b: d_widen(e, b), "ds": lambda e, b, t: d_shuffle(e, b, t), "dt": lambda e, q: d_transpose(q),
+            "bb": lambda e, n: b3_spread(), "bc": lambda e, n: copy(e, b3t[:], w_bank["b3"][:]),
+            "ws": w_shuffle, "wt": lambda e, i, j: w_transpose(i, j), "wc": w_copy,
+            "w2q": lambda e, j: w2_quant(j), "w3q": lambda e, k: w3_quant(k),
+            "xt": lambda e, n: x_transpose(n), "xc": x_copy, "xq": lambda e, q: x_quant(q),
+            "wid": d_widen, "ds": d_shuffle, "dt": lambda e, q: d_transpose(q),
             "dc": lambda e, q: d_scale(q), "dq": lambda e, q: d_quant(q), "S2": lambda e, q, a: stage2(q, a),
-            "E": lambda e, q, t: h_relu(e, q, t), "hi": lambda e, q: h_interleave(e, q), "hq": lambda e, q: h_quant(q),
-            "U": lambda e, n: stage3(n), "F": lambda e, n: add_residual(n), "r": lambda e, b, g: residual(e, b, g),
-            "R": lambda e, b, h, o0, o1: finish(e, b, h, o0, o1),
+            "E": h_relu, "hi": h_interleave, "hq": lambda e, q: h_quant(q),
+            "U": lambda e, n: stage3(n), "F": lambda e, n: add_residual(n), "r": lambda e, b, h: residual(b, h), "R": finish,
         }
         for word in SEQ.split():
             parts = word.split(":")

@@ -16,24 +16,37 @@ RELU = mybir.ActivationFunctionType.Relu
 P = 128
 N, ND, NP, KW = 256, 512, 6, 3
 JETS = 2 * NP
+HALF = ND // 2
 FLOPS = 2 * 2 * N * NP * KW * ND * ND
-GROUPS = [(0, 0), (0, 1), (0, 2), (1, 2), (1, 0), (1, 1), (2, 0), (2, 1), (2, 2), (3, 2), (3, 0), (3, 1)]
-POS = {g: n for n, g in enumerate(GROUPS)}
 
-GROUP_SIZES = [2, 4, 2, 4]
-SEQ = """
-ws:V:0,0,0,64 ws:S:0,0,64,128 wid:V:0 wt:T:0,0 ws:S:0,1,0,128 bb:T:0 ws:V:0,2,0,128 ds:V:0 bc:S:0 wt:T:0,2 wc:S:0,0
-wt:T:0,1 ws:V:0,3,0,128 dt:T:2 wc:S:0,2 wt:T:0,3 dc:V:2 wc:S:0,1 wt:T:0,5 wc:S:0,3 wt:T:0,4 w2q:V:0 dt:T:1 wc:S:0,5
-w2q:V:1 xt:T:0 wc:S:0,4 dc:V:1 ws:S:1,0,0,128 xt:T:5 ws:V:1,1,0,128 dt:T:0 xt:T:4 xc:S:5 ws:V:1,3,0,128 ws:V:1,2,0,128
-xc:S:0 xt:T:1 dc:V:0 xc:S:4 wt:T:1,4 dq:V:1 xt:T:3 wc:S:1,4 wid:V:1 xc:S:1 xt:T:2 xc:S:3 wt:T:1,3 r:V:0,1 wt:T:1,5
-wc:S:1,3 xt:T:11 xc:S:2 xq:V:0 xt:T:8 w2q:V:2 wc:S:1,5 xt:T:9 xq:V:1 ds:S:1 xt:T:10 dq:V:0 xc:V:8 xc:S:9 S2:T:1,0
-r:V:0,0 xc:S:11 dt:T:5 S2:T:0,0 dc:V:5 xc:S:10 dt:T:3 wt:T:1,0 r:V:1,1 E:S:1,0 dt:T:4 wt:T:1,1 E:S:0,1 S2:T:0,1
-E:S:0,0 wc:S:1,0 dc:V:4 S2:T:1,1 E:S:0,2 E:S:0,3 wt:T:1,2 dc:V:3 wc:S:1,1 xt:T:7 E:S:1,1 xq:V:3 S2:T:1,3 wc:S:1,2
-hi:S:0 S2:T:1,2 w3q:V:2 xt:T:6 dq:V:3 E:S:1,3 w3q:V:1 E:S:1,2 S2:T:3,3 w3q:V:0 xc:S:6 hq:V:0 S2:T:3,1 dq:V:2 hi:V:1
-E:S:3,3 U:T:0 E:S:3,1 S2:T:3,0 xc:S:7 F:V:0 S2:T:3,2 hq:V:1 U:T:3 E:S:3,0 xq:V:2 E:S:3,2 U:T:5 F:V:3 S2:T:2,0 hi:S:3
-r:V:1,0 U:T:4 S2:T:2,1 F:V:5 F:V:4 U:T:1 E:S:2,1 E:S:2,2 hq:V:3 U:T:2 E:S:2,3 F:V:1 E:S:2,0 R:S:0,1,0,256 U:T:10
-hi:V:2 F:V:2 hq:V:2 U:T:11 R:S:0,0,0,256 F:V:10 U:T:9 F:V:11 U:T:7 F:V:9 U:T:8 F:V:7 R:S:1,1,0,100 R:V:1,1,100,256
-U:T:6 F:V:8 F:V:6 R:S:1,0,0,100 R:V:1,0,100,256
+PIECES = [(o + d, k) for o in (0, 2) for d, k in ((0, 0), (0, 1), (0, 2), (1, 2), (1, 0), (1, 1))]
+PLACE_OF = {piece: n for n, piece in enumerate(PIECES)}
+
+GROUP_SIZES = [2, 4, 4, 2]
+STARTS = [sum(GROUP_SIZES[:q]) for q in range(len(GROUP_SIZES))]
+GROUP_OF = {STARTS[q] + r: (q, r) for q in range(len(GROUP_SIZES)) for r in range(GROUP_SIZES[q])}
+
+ORDER = """
+w_shuffle:V:0,0,0,64 w_shuffle:S:0,0,64,128 d_widen:V:0 w_turn:T:0,0 b3_spread:T: w_copy:S:0,0 w_shuffle:V:0,1,0,128
+d_turn:T:1 b3_copy:S: w_shuffle:V:0,2,0,128 w_shuffle:S:0,3,0,128 w_turn:T:0,2 w_turn:T:0,1 d_scale:V:1 d_turn:T:0
+w_copy:S:0,2 w_turn:T:0,3 d_scale:V:0 w_turn:T:0,4 w_copy:S:0,3 w_turn:T:0,5 w_copy:S:0,1 d_turn:T:2 w2_quant:V:1
+w_copy:S:0,4 d_quant:V:0 x_turn:T:3 w_copy:S:0,5 w2_quant:V:0 w_shuffle:S:1,1,0,128 d_scale:V:2 x_turn:T:2
+w2_quant:V:2 x_turn:T:0 w_shuffle:V:1,3,0,128 x_copy:S:2 x_turn:T:1 d_widen:V:1 x_copy:S:0 x_turn:T:5 x_copy:S:1
+x_turn:T:4 residual:V:0,0 x_copy:S:3 d_turn:T:3 w_shuffle:V:1,0,0,128 d_turn:T:4 x_copy:S:5 x_quant:V:0 x_turn:T:8
+x_copy:S:4 d_scale:V:3 x_turn:T:7 w_shuffle:S:1,2,0,128 d_scale:V:4 x_turn:T:6 x_quant:V:1 x_turn:T:10 x_copy:S:8
+residual:V:0,1 x_turn:T:9 x_copy:S:7 x_turn:T:11 residual:V:1,0 x_copy:S:6 stage2:T:0,0 x_copy:S:10 d_quant:V:2
+x_copy:V:9 w_turn:T:1,0 x_copy:S:11 w_turn:T:1,3 w_turn:T:1,1 w_turn:T:1,4 d_quant:V:1 w_copy:S:1,3 w_turn:T:1,2
+w_turn:T:1,5 x_quant:V:2 w_copy:S:1,1 d_turn:T:5 w_copy:S:1,2 residual:V:1,1 stage2:T:1,0 w_copy:S:1,5 w_copy:S:1,4
+stage2:T:1,3 h_relu:S:0,0 d_scale:V:5 stage2:T:1,1 h_relu:S:1,0 w_copy:S:1,0 stage2:T:1,2 h_relu:S:1,1 stage2:T:2,1
+w3_quant:V:0 h_relu:S:1,2 d_quant:V:3 stage2:T:2,3 h_relu:S:1,3 w3_quant:V:2 stage2:T:2,0 x_quant:V:3 h_relu:S:0,1
+h_relu:S:2,1 h_lay:V:1 stage2:T:2,2 h_relu:S:2,0 stage2:T:0,1 h_relu:S:2,3 w3_quant:V:1 stage2:T:3,1 h_relu:S:2,2
+h_quant:V:1 h_relu:S:0,3 stage2:T:3,0 h_lay:V:2 h_relu:S:0,2 stage3:T:4 h_lay:S:0 stage3:T:2 add:V:4,0,256
+h_relu:S:3,0 stage3:T:5 h_quant:V:0 h_relu:S:3,2 h_quant:V:2 h_relu:S:3,1 stage3:T:1 h_relu:S:3,3 add:V:2,0,256
+stage3:T:0 h_lay:S:3 add:V:1,0,256 stage3:T:3 add:V:0,0,256 stage3:T:6 add:V:5,0,256 finish:S:0,0,128,256 h_quant:V:3
+stage3:T:7 add:V:3,0,256 finish:S:0,0,0,128 stage3:T:8 add:V:6,128,256 add:V:7,0,256 finish:S:0,1,0,128 stage3:T:11
+add:V:8,0,256 finish:S:0,1,128,256 stage3:T:10 add:V:6,0,128 add:V:11,0,256 finish:S:1,0,192,256 stage3:T:9
+add:V:10,0,256 finish:S:1,0,0,64 finish:S:1,0,64,128 add:V:9,128,256 finish:S:1,0,128,192 add:V:9,0,128
+finish:S:1,1,192,256 finish:V:1,1,128,192 finish:V:1,1,64,128 finish:S:1,1,0,64
 """
 
 
@@ -42,38 +55,40 @@ def tile_dijetresnetblock_pa_kernel(tc, x, d_h1_bytes, d_h1_scale, d1, W2, b2, W
     with ExitStack() as ctx:
         keep = ctx.enter_context(tc.tile_pool(name="keep", bufs=1))
         work = ctx.enter_context(tc.tile_pool(name="work", bufs=2))
-        ptr = ctx.enter_context(tc.psum_pool(name="ptr", bufs=4))
-        ps2 = ctx.enter_context(tc.psum_pool(name="ps2", bufs=2))
-        ps3 = ctx.enter_context(tc.psum_pool(name="ps3", bufs=2))
+        psum = ctx.enter_context(tc.psum_pool(name="psum", bufs=8))
         ctx.enter_context(tc.manual_schedule())
+        rows = [slice(b * P, (b + 1) * P) for b in range(2)]
+
+        def new_bank():
+            bank = psum.tile([P, 512], F32, name="bank")
+            return bank
+
+        def copy(engine, out_ap, in_ap):
+            if engine == "S":
+                nc.scalar.copy(out=out_ap, in_=in_ap)
+            else:
+                nc.vector.tensor_copy(out=out_ap, in_=in_ap)
 
         w_raw = [[keep.tile([P, 2, ND * KW], BF16, name="w_raw%d_%d" % (i, n), tag="raw%d_%d" % (i, n)) for n in range(2)] for i in range(2)]
         w_src = [W2.rearrange("(m t) i k -> m t (i k)", t=4), W3.rearrange("(t m) i k -> m t (i k)", t=4)]
         x_raw = [keep.tile([P, ND * JETS], BF16, name="x_raw%d" % b) for b in range(2)]
-        d_byt = [keep.tile([P, ND * NP], U8, name="d_byt%d" % b) for b in range(2)]
-        d_raw = [keep.tile([P, ND * NP], BF16, name="d_raw%d" % b, tag="d_raw") for b in range(2)]
+        d_bytes = [keep.tile([P, ND * NP], U8, name="d_bytes%d" % b) for b in range(2)]
         d1_raw = [keep.tile([P, ND, NP], BF16, name="d1_raw%d" % b, tag="raw0_%d" % b) for b in range(2)]
-        res = [[keep.tile([P, 3, 256, 2], F32, name="res%d_%d" % (b, h), tag="res%d" % h if b == 0 else "raw1_%d" % h) for h in range(2)] for b in range(2)]
-        sc = keep.tile([P, 4], F32, name="sc")
-        b2t = keep.tile([P, 4], BF16, name="b2t")
-        b2f = keep.tile([P, 4], F32, name="b2f")
+        d_scale = keep.tile([P, 4], F32, name="d_scale")
+        b2_raw = keep.tile([P, 4], BF16, name="b2_raw")
+        b2_col = keep.tile([P, 4], F32, name="b2_col")
         b3_row = keep.tile([P, ND], BF16, name="b3_row")
-        b3t = keep.tile([P, ND], F32, name="b3t")
+        b3_all = keep.tile([P, ND], F32, name="b3_all")
         ones = keep.tile([P, P], BF16, name="ones")
-        rows = [slice(b * P, (b + 1) * P) for b in range(2)]
 
-        def load_w(i, t):
-            nc.sync.dma_start(out=w_raw[i][t // 2][:, t % 2, :], in_=w_src[i][:, t, :])
+        def load_w(i, o):
+            nc.sync.dma_start(out=w_raw[i][o // 2][:, o % 2, :], in_=w_src[i][:, o, :])
 
         def load_x(b):
             nc.sync.dma_start(out=x_raw[b][:], in_=x[rows[b]].rearrange("b i j -> b (i j)"))
 
         def load_d(b):
-            nc.sync.dma_start(out=d_byt[b][:], in_=d_h1_bytes[rows[b]].rearrange("b i s -> b (i s)"))
-
-        def load_small():
-            nc.sync.dma_start(out=sc[:], in_=d_h1_scale.rearrange("o (p t) w -> p (o t w)", t=4))
-            nc.sync.dma_start(out=b3_row[0:1, :], in_=b3.unsqueeze(0))
+            nc.sync.dma_start(out=d_bytes[b][:], in_=d_h1_bytes[rows[b]].rearrange("b i s -> b (i s)"))
 
         nc.vector.memset(b3_row[:], 0.0)
         nc.vector.memset(ones[:], 1.0)
@@ -81,13 +96,14 @@ def tile_dijetresnetblock_pa_kernel(tc, x, d_h1_bytes, d_h1_scale, d1, W2, b2, W
             cols = slice(c * ND * KW // 2, (c + 1) * ND * KW // 2)
             nc.sync.dma_start(out=w_raw[0][0][:, 0, cols], in_=w_src[0][:, 0, cols])
         load_d(0)
-        load_small()
-        for t in range(1, 4):
-            load_w(0, t)
+        nc.sync.dma_start(out=d_scale[:], in_=d_h1_scale.rearrange("o (p t) w -> p (o t w)", t=4))
+        nc.sync.dma_start(out=b3_row[0:1, :], in_=b3.unsqueeze(0))
+        for o in range(1, 4):
+            load_w(0, o)
         load_x(0)
-        nc.sync.dma_start(out=b2t[:], in_=b2.rearrange("(p t) -> p t", t=4))
-        for t in range(4):
-            load_w(1, t)
+        nc.sync.dma_start(out=b2_raw[:], in_=b2.rearrange("(p t) -> p t", t=4))
+        for o in range(4):
+            load_w(1, o)
         load_d(1)
         nc.sync.dma_start(out=d1_raw[0][:], in_=d1[rows[0]])
         load_x(1)
@@ -98,32 +114,16 @@ def tile_dijetresnetblock_pa_kernel(tc, x, d_h1_bytes, d_h1_scale, d1, W2, b2, W
         warm = keep.tile([P, 1], F32, name="warm")
         nc.vector.memset(warm[:], 0.0)
         nc.scalar.activation(out=warm[:], in_=warm[:], func=RELU)
-        nc.gpsimd.tensor_copy(out=b2f[:], in_=b2t[:])
-
-        def copy(engine, out_ap, in_ap):
-            if engine == "S":
-                nc.scalar.copy(out=out_ap, in_=in_ap)
-            else:
-                nc.vector.tensor_copy(out=out_ap, in_=in_ap)
-
-        def b3_spread():
-            bank = ptr.tile([P, ND], F32, name="bank")
-            nc.tensor.matmul(bank[:], lhsT=ones[:], rhs=b3_row[:], start=True, stop=True)
-            w_bank["b3"] = bank
-
-        def residual(b, half):
-            o = slice(half * 256, half * 256 + 256)
-            nc.vector.tensor_tensor(out=res[b][half][:], in0=d1_raw[b][:, o, :].rearrange("b o (g s) -> b g o s", s=2),
-                                    in1=b3t[:, o].unsqueeze(1).unsqueeze(3).to_broadcast([P, 3, 256, 2]), op=ADD)
+        nc.gpsimd.tensor_copy(out=b2_col[:], in_=b2_raw[:])
 
         w_sh = [[keep.tile([P, KW, 2, P, 2], BF16, name="w_sh%d_%d" % (i, o), tag="w_sh%d" % o) for o in range(4)] for i in range(2)]
-        w2_g = keep.tile([P, 12, P, 2], F32, name="w2_g", align_bytes=64)
+        w2_g = keep.tile([P, 12, P, 2], F32, name="w2_g", tag="w2_g", align_bytes=64)
         w2_c = keep.tile([P, 12, P], U32, name="w2_c", align_bytes=64)
         w2_s = keep.tile([P, 12, P], U8, name="w2_s", align_bytes=64)
         w3_g = keep.tile([P, KW, ND, 2], F32, name="w3_g", align_bytes=64)
         w3_c = keep.tile([P, KW, ND], U32, name="w3_c", align_bytes=64)
         w3_s = keep.tile([P, KW, ND], U8, name="w3_s", align_bytes=64)
-        w_bank = {}
+        banks = {}
 
         def w_shuffle(engine, i, o, p0, p1):
             src = w_raw[i][o // 2][:, o % 2, :].rearrange("m (p u e k) -> m u p k e", u=2, e=2, k=KW)[:, :, p0:p1]
@@ -134,164 +134,167 @@ def tile_dijetresnetblock_pa_kernel(tc, x, d_h1_bytes, d_h1_scale, d1, W2, b2, W
                 for u in range(2):
                     nc.scalar.copy(out=dst[:, u], in_=src[:, u])
 
-        def w_transpose(i, j):
-            bank = ptr.tile([P, 2, 2, P], F32, name="bank")
+        def w_transpose(engine, i, j):
+            bank = new_bank()
+            view = bank[:].rearrange("p (n u m) -> p n u m", n=2, u=2)
             for n in range(2):
-                o, k = GROUPS[2 * j + n]
+                o, k = PIECES[2 * j + n]
                 for u in range(2):
-                    nc.tensor.transpose(bank[:, n, u, :], w_sh[i][o][:, k, u].rearrange("m p e -> m (p e)").bitcast(F32), ident[:])
-            w_bank[i, j] = bank
+                    nc.tensor.transpose(view[:, n, u, :], w_sh[i][o][:, k, u].rearrange("m p e -> m (p e)").bitcast(F32), ident[:])
+            banks["w", i, j] = bank
 
         def w_copy(engine, i, j):
-            src = w_bank[i, j][:].rearrange("p n u m -> p n m u")
+            src = banks["w", i, j][:].rearrange("p (n u m) -> p n m u", n=2, u=2)
+            (oa, ka), (ob, kb) = PIECES[2 * j], PIECES[2 * j + 1]
             if i == 0:
-                copy(engine, w2_g[:, 2 * j : 2 * j + 2], src)
-                return
-            (oa, ka), (ob, kb) = GROUPS[2 * j], GROUPS[2 * j + 1]
-            if oa == ob:
-                copy(engine, w3_g[:, ka : ka + 2, oa * P : (oa + 1) * P, :], src)
+                dst = w2_g[:, 2 * j : 2 * j + 2]
+            elif oa == ob:
+                dst = w3_g[:, ka : ka + 2, oa * P : (oa + 1) * P, :]
             else:
-                copy(engine, w3_g[:, ka, oa * P : (oa + 2) * P, :].rearrange("p (n m) u -> p n m u", n=2), src)
+                dst = w3_g[:, ka, oa * P : (oa + 2) * P, :].rearrange("p (n m) u -> p n m u", n=2)
+            copy(engine, dst, src)
 
-        def w2_quant(j):
+        def w2_quantise(engine, j):
             g = slice(4 * j, 4 * j + 4)
             nc.vector.quantize_mx(
                 out=w2_c[:, g, :].rearrange("p n m -> p (n m)").bitcast(FP8X4),
                 scales=w2_s[:, g, :].rearrange("p n m -> p (n m)"),
                 in_=w2_g[:, g, :, :].rearrange("p n m u -> p (n m u)").bitcast(BF16))
 
-        def w3_quant(k):
+        def w3_quantise(engine, k):
             nc.vector.quantize_mx(out=w3_c[:, k, :].bitcast(FP8X4), scales=w3_s[:, k, :],
                                   in_=w3_g[:, k, :, :].rearrange("p m u -> p (m u)").bitcast(BF16))
 
-        starts = [sum(GROUP_SIZES[:q]) for q in range(len(GROUP_SIZES))]
-        group_of = {}
-        for q in range(len(GROUP_SIZES)):
-            for n in range(starts[q], starts[q] + GROUP_SIZES[q]):
-                group_of[n] = (q, n - starts[q])
+        res = [[keep.tile([P, 3, HALF, 2], F32, name="res%d_%d" % (b, h), tag="res%d" % h if b == 0 else "raw1_%d" % h) for h in range(2)] for b in range(2)]
+
+        def b3_spread(engine):
+            bank = new_bank()
+            nc.tensor.matmul(bank[:], lhsT=ones[:], rhs=b3_row[:], start=True, stop=True)
+            banks["b3"] = bank
+
+        def b3_copy(engine):
+            copy(engine, b3_all[:], banks["b3"][:])
+
+        def residual(engine, b, half):
+            o = slice(half * HALF, (half + 1) * HALF)
+            nc.vector.tensor_tensor(out=res[b][half][:], in0=d1_raw[b][:, o, :].rearrange("b o (g s) -> b g o s", s=2),
+                                    in1=b3_all[:, o].unsqueeze(1).unsqueeze(3).to_broadcast([P, 3, HALF, 2]), op=ADD)
+
         x_c = [keep.tile([P, 2, z * P], U32, name="x_c%d" % q, align_bytes=64) for q, z in enumerate(GROUP_SIZES)]
         x_s = [keep.tile([P, 2, z * P], U8, name="x_s%d" % q, align_bytes=64) for q, z in enumerate(GROUP_SIZES)]
         d_c = [keep.tile([P, z * P], U32, name="d_c%d" % q, align_bytes=64) for q, z in enumerate(GROUP_SIZES)]
         d_s = [keep.tile([P, z * P], U8, name="d_s%d" % q, align_bytes=64) for q, z in enumerate(GROUP_SIZES)]
         h_c = [keep.tile([P, z * P], U32, name="h_c%d" % q, align_bytes=64) for q, z in enumerate(GROUP_SIZES)]
         h_s = [keep.tile([P, z * P], U8, name="h_s%d" % q, align_bytes=64) for q, z in enumerate(GROUP_SIZES)]
-        d_sh = [keep.tile([P, 3, 4, P], F32, name="d_sh%d" % b) for b in range(2)]
-        x_bank, d_bank, x_g, d_g, acc2, h_p, h_g, acc3, sums = {}, {}, {}, {}, {}, {}, {}, {}, {}
+        x_g, d_g, h_p, h_g, acc2 = {}, {}, {}, {}, {}
 
-        def x_transpose(n):
-            b, s = n // 6, n % 6
-            bank = ptr.tile([P, 4, P], F32, name="bank")
-            view = x_raw[b][:].bitcast(F32).rearrange("b (p t s) -> b t s p", t=4, s=NP)
+        def x_transpose(engine, n):
+            b, s = n // NP, n % NP
+            bank = new_bank()
+            words = x_raw[b][:].bitcast(F32).rearrange("b (p t s) -> b t s p", t=4, s=NP)
             for t in range(4):
-                nc.tensor.transpose(bank[:, t, :], view[:, t, s, :], ident[:])
-            x_bank[n] = bank
+                nc.tensor.transpose(bank[:, t * P : (t + 1) * P], words[:, t, s, :], ident[:])
+            banks["x", n] = bank
 
         def x_copy(engine, n):
-            q, r = group_of[n]
+            q, r = GROUP_OF[n]
             if q not in x_g:
-                x_g[q] = work.tile([P, 2, GROUP_SIZES[q] * P, 4], BF16, name="xg", bufs=2, align_bytes=64)
-            copy(engine, x_g[q][:, :, r * P : (r + 1) * P, :], x_bank[n][:].bitcast(BF16).rearrange("p t (b k) -> p k b t", k=2))
+                x_g[q] = work.tile([P, 2, GROUP_SIZES[q] * P, 4], BF16, name="xg", align_bytes=64)
+            copy(engine, x_g[q][:, :, r * P : (r + 1) * P, :], banks["x", n][:].bitcast(BF16).rearrange("p (t b k) -> p k b t", t=4, k=2))
 
-        def x_quant(q):
+        def x_quantise(engine, q):
             nc.vector.quantize_mx(out=x_c[q][:].rearrange("p k n -> p (k n)").bitcast(FP8X4),
                                   scales=x_s[q][:].rearrange("p k n -> p (k n)"),
                                   in_=x_g[q][:].rearrange("p k n t -> p (k n t)"))
 
+        d_raw = [keep.tile([P, ND * NP], BF16, name="d_raw%d" % b) for b in range(2)]
+
         def d_widen(engine, b):
-            copy(engine, d_raw[b][:], d_byt[b][:].bitcast(FP8))
+            copy(engine, d_raw[b][:], d_bytes[b][:].bitcast(FP8))
 
-        def d_shuffle(engine, b):
-            copy(engine, d_sh[b][:].rearrange("b q t p -> b t p q"), d_raw[b][:].bitcast(F32).rearrange("b (p t q) -> b t p q", t=4, q=3))
-
-        def d_transpose(pair):
-            bank = ptr.tile([P, 4, P], F32, name="bank")
+        def d_transpose(engine, pair):
+            b, g = pair // 3, pair % 3
+            words = d_raw[b][:].bitcast(F32).rearrange("b (p t g) -> b g t p", t=4, g=3)
+            bank = new_bank()
             for t in range(4):
-                nc.tensor.transpose(bank[:, t, :], d_sh[pair // 3][:, pair % 3, t, :], ident[:])
-            d_bank[pair] = bank
+                nc.tensor.transpose(bank[:, t * P : (t + 1) * P], words[:, g, t, :], ident[:])
+            banks["d", pair] = bank
 
-        def d_scale(pair):
-            q, r = group_of[2 * pair]
+        def d_multiply(engine, pair):
+            q, r = GROUP_OF[2 * pair]
             if q not in d_g:
                 d_g[q] = work.tile([P, GROUP_SIZES[q] * P, 4], BF16, name="dg", align_bytes=64)
             nc.vector.tensor_tensor(
                 out=d_g[q][:, r * P : (r + 2) * P, :].rearrange("p (s b) t -> p s b t", s=2),
-                in0=d_bank[pair][:].bitcast(BF16).rearrange("p t (b s) -> p s b t", s=2),
-                in1=sc[:].unsqueeze(1).unsqueeze(1).to_broadcast([P, 2, P, 4]), op=MULT)
+                in0=banks["d", pair][:].bitcast(BF16).rearrange("p (t b s) -> p s b t", t=4, s=2),
+                in1=d_scale[:].unsqueeze(1).unsqueeze(1).to_broadcast([P, 2, P, 4]), op=MULT)
 
-        def d_quant(q):
+        def d_quantise(engine, q):
             nc.vector.quantize_mx(out=d_c[q][:].bitcast(FP8X4), scales=d_s[q][:], in_=d_g[q][:].rearrange("p n t -> p (n t)"))
 
-        def stage2(q, a):
-            z = GROUP_SIZES[q]
-            per = 4 // z
-            acc = ps2.tile([P, per, z * P], F32, name="acc2")
-            for n in range(per):
+        def first_stage(engine, q, a):
+            width = GROUP_SIZES[q] * P
+            bank = new_bank()
+            for n in range(512 // width):
+                t = (512 // width) * a + n
+                acc2[q, t] = bank[:, n * width : (n + 1) * width]
                 for k in range(KW):
-                    g = POS[(per * a + n, k)]
-                    rhs = x_c[q][:, k] if k < 2 else d_c[q][:]
-                    rhs_s = x_s[q][:, k] if k < 2 else d_s[q][:]
-                    nc.tensor.matmul_mx(out=acc[:, n, :], lhsT=w2_c[:, g, :].bitcast(FP8X4), lhsT_scale=w2_s[:, g, :],
-                                        rhs=rhs.bitcast(FP8X4), rhs_scale=rhs_s, start=(k == 0), stop=(k == 2))
-                acc2[q, per * a + n] = acc[:, n, :]
+                    g = PLACE_OF[t, k]
+                    rhs, rhs_scale = (x_c[q][:, k], x_s[q][:, k]) if k < 2 else (d_c[q][:], d_s[q][:])
+                    nc.tensor.matmul_mx(out=acc2[q, t], lhsT=w2_c[:, g, :].bitcast(FP8X4), lhsT_scale=w2_s[:, g, :],
+                                        rhs=rhs.bitcast(FP8X4), rhs_scale=rhs_scale, start=(k == 0), stop=(k == 2))
 
         def h_relu(engine, q, t):
             if q not in h_p:
-                h_p[q] = work.tile([P, 4, GROUP_SIZES[q] * P], BF16, name="hp")
-            if engine == "S":
-                nc.scalar.activation(out=h_p[q][:, t, :], in_=acc2[q, t], func=RELU, bias=b2f[:, t : t + 1])
-            else:
-                nc.vector.tensor_scalar(out=h_p[q][:, t, :], in0=acc2[q, t], scalar1=b2f[:, t : t + 1], scalar2=0.0,
-                                        op0=ADD, op1=mybir.AluOpType.max)
+                h_p[q] = work.tile([P, 4, GROUP_SIZES[q] * P], BF16, name="hp", bufs=3)
+            nc.scalar.activation(out=h_p[q][:, t, :], in_=acc2[q, t], func=RELU, bias=b2_col[:, t : t + 1])
 
         def h_interleave(engine, q):
-            h_g[q] = work.tile([P, GROUP_SIZES[q] * P, 4], BF16, name="hg", align_bytes=64)
+            h_g[q] = work.tile([P, GROUP_SIZES[q] * P, 4], BF16, name="hg", bufs=3, align_bytes=64)
             copy(engine, h_g[q][:].rearrange("p (c i) t -> p c t i", i=4), h_p[q][:].rearrange("p t (c i) -> p c t i", i=4))
 
-        def h_quant(q):
+        def h_quantise(engine, q):
             nc.vector.quantize_mx(out=h_c[q][:].bitcast(FP8X4), scales=h_s[q][:], in_=h_g[q][:].rearrange("p n t -> p (n t)"))
 
-        def stage3(n):
+        sums = [keep.tile([P, 2, 3, HALF, 2], F32, name="sums%d" % b, tag="sums" if b == 0 else "w2_g", align_bytes=64) for b in range(2)]
+        result = [keep.tile([P, ND, NP], F32, name="result%d" % b, tag="result" if b == 0 else "x_raw0") for b in range(2)]
+
+        def second_stage(engine, n):
             b, half, g = n // 6, (n % 6) // 3, n % 3
-            acc = ps3.tile([P, 2, 256], F32, name="acc3")
-            o = slice(half * 256, half * 256 + 256)
+            o = slice(half * HALF, (half + 1) * HALF)
+            bank = new_bank()
             for s in range(2):
-                q, r = group_of[6 * b + 2 * g + s]
+                q, r = GROUP_OF[NP * b + 2 * g + s]
                 c = slice(r * P, (r + 1) * P)
                 for k in range(KW):
-                    lhs = x_c[q][:, k, c] if k < 2 else h_c[q][:, c]
-                    lhs_s = x_s[q][:, k, c] if k < 2 else h_s[q][:, c]
-                    nc.tensor.matmul_mx(out=acc[:, s, :], lhsT=lhs.bitcast(FP8X4), lhsT_scale=lhs_s,
-                                        rhs=w3_c[:, k, o].bitcast(FP8X4), rhs_scale=w3_s[:, k, o],
-                                        start=(k == 0), stop=(k == 2))
-            acc3[n] = acc
+                    lhs, lhs_scale = (x_c[q][:, k, c], x_s[q][:, k, c]) if k < 2 else (h_c[q][:, c], h_s[q][:, c])
+                    nc.tensor.matmul_mx(out=bank[:, s * HALF : (s + 1) * HALF], lhsT=lhs.bitcast(FP8X4), lhsT_scale=lhs_scale,
+                                        rhs=w3_c[:, k, o].bitcast(FP8X4), rhs_scale=w3_s[:, k, o], start=(k == 0), stop=(k == 2))
+            banks["out", n] = bank
 
-        def add_residual(n):
+        def add_residual(engine, n, o0, o1):
             b, half, g = n // 6, (n % 6) // 3, n % 3
-            if (b, half) not in sums:
-                sums[b, half] = work.tile([P, 3, 256, 2], F32, name="sums")
-            nc.vector.tensor_tensor(out=sums[b, half][:, g], in0=acc3[n][:].rearrange("p s o -> p o s"),
-                                    in1=res[b][half][:, g], op=ADD)
+            nc.vector.tensor_tensor(out=sums[b][:, half, g, o0:o1], in0=banks["out", n][:].rearrange("p (s o) -> p o s", s=2)[:, o0:o1],
+                                    in1=res[b][half][:, g, o0:o1], op=ADD)
 
         def finish(engine, b, half, o0, o1):
-            fin = work.tile([P, o1 - o0, NP], F32, name="fin%d_%d_%d" % (b, half, o0), tag="fin", bufs=2)
-            dst = fin[:].rearrange("p o (g s) -> p o g s", s=2)
-            src = sums[b, half][:, :, o0:o1, :].rearrange("p g o s -> p o g s")
+            o = slice(half * HALF + o0, half * HALF + o1)
+            dst = result[b][:, o, :].rearrange("p o (g s) -> p o g s", s=2)
+            src = sums[b][:, half, :, o0:o1, :].rearrange("p g o s -> p o g s")
             if engine == "S":
                 nc.scalar.activation(out=dst, in_=src, func=RELU)
             else:
                 nc.vector.tensor_scalar_max(out=dst, in0=src, scalar1=0.0)
-            nc.sync.dma_start(out=out[rows[b], half * 256 + o0 : half * 256 + o1, :], in_=fin[:])
+            nc.sync.dma_start(out=out[rows[b], o, :], in_=result[b][:, o, :])
 
-        table = {
-            "bb": lambda e, n: b3_spread(), "bc": lambda e, n: copy(e, b3t[:], w_bank["b3"][:]),
-            "ws": w_shuffle, "wt": lambda e, i, j: w_transpose(i, j), "wc": w_copy,
-            "w2q": lambda e, j: w2_quant(j), "w3q": lambda e, k: w3_quant(k),
-            "xt": lambda e, n: x_transpose(n), "xc": x_copy, "xq": lambda e, q: x_quant(q),
-            "wid": d_widen, "ds": d_shuffle, "dt": lambda e, q: d_transpose(q),
-            "dc": lambda e, q: d_scale(q), "dq": lambda e, q: d_quant(q), "S2": lambda e, q, a: stage2(q, a),
-            "E": h_relu, "hi": h_interleave, "hq": lambda e, q: h_quant(q),
-            "U": lambda e, n: stage3(n), "F": lambda e, n: add_residual(n), "r": lambda e, b, h: residual(b, h), "R": finish,
+        STEPS = {
+            "w_shuffle": w_shuffle, "w_turn": w_transpose, "w_copy": w_copy, "w2_quant": w2_quantise, "w3_quant": w3_quantise,
+            "b3_spread": b3_spread, "b3_copy": b3_copy, "residual": residual,
+            "x_turn": x_transpose, "x_copy": x_copy, "x_quant": x_quantise,
+            "d_widen": d_widen, "d_turn": d_transpose, "d_scale": d_multiply, "d_quant": d_quantise,
+            "stage2": first_stage, "h_relu": h_relu, "h_lay": h_interleave, "h_quant": h_quantise,
+            "stage3": second_stage, "add": add_residual, "finish": finish,
         }
-        for word in SEQ.split():
-            parts = word.split(":")
-            table[parts[0]](parts[1], *[int(v) for v in parts[2].split(",")])
+        for entry in ORDER.split():
+            name, engine, arguments = entry.split(":")
+            STEPS[name](engine, *[int(v) for v in arguments.split(",") if v])

from contextlib import ExitStack

import concourse.mybir as mybir
from concourse.masks import make_identity

F32 = mybir.dt.float32
BF16 = mybir.dt.bfloat16
U8 = mybir.dt.uint8
U32 = mybir.dt.uint32
FP8 = mybir.dt.float8_e4m3fn
FP8X4 = mybir.dt.float8_e4m3fn_x4
ADD = mybir.AluOpType.add
MULT = mybir.AluOpType.mult
RELU = mybir.ActivationFunctionType.Relu

P = 128
N, ND, NP, KW = 256, 512, 6, 3
JETS = 2 * NP
HALF = ND // 2
FLOPS = 2 * 2 * N * NP * KW * ND * ND

PIECES = [(o + d, k) for o in (0, 2) for d, k in ((0, 0), (0, 1), (0, 2), (1, 2), (1, 0), (1, 1))]
PLACE_OF = {piece: n for n, piece in enumerate(PIECES)}

GROUP_SIZES = [2, 4, 4, 2]
STARTS = [sum(GROUP_SIZES[:q]) for q in range(len(GROUP_SIZES))]
GROUP_OF = {STARTS[q] + r: (q, r) for q in range(len(GROUP_SIZES)) for r in range(GROUP_SIZES[q])}

ORDER = """
w_shuffle:V:0,0,0,64 w_shuffle:S:0,0,64,128 d_widen:V:0 w_turn:T:0,0 b3_spread:T: w_copy:S:0,0 w_shuffle:V:0,1,0,128
d_turn:T:1 b3_copy:S: w_shuffle:V:0,2,0,128 w_shuffle:S:0,3,0,128 w_turn:T:0,2 w_turn:T:0,1 d_scale:V:1 d_turn:T:0
w_copy:S:0,2 w_turn:T:0,3 d_scale:V:0 w_turn:T:0,4 w_copy:S:0,3 w_turn:T:0,5 w_copy:S:0,1 d_turn:T:2 w2_quant:V:1
w_copy:S:0,4 d_quant:V:0 x_turn:T:3 w_copy:S:0,5 w2_quant:V:0 w_shuffle:S:1,1,0,128 d_scale:V:2 x_turn:T:2
w2_quant:V:2 x_turn:T:0 w_shuffle:V:1,3,0,128 x_copy:S:2 x_turn:T:1 d_widen:V:1 x_copy:S:0 x_turn:T:5 x_copy:S:1
x_turn:T:4 residual:V:0,0 x_copy:S:3 d_turn:T:3 w_shuffle:V:1,0,0,128 d_turn:T:4 x_copy:S:5 x_quant:V:0 x_turn:T:8
x_copy:S:4 d_scale:V:3 x_turn:T:7 w_shuffle:S:1,2,0,128 d_scale:V:4 x_turn:T:6 x_quant:V:1 x_turn:T:10 x_copy:S:8
residual:V:0,1 x_turn:T:9 x_copy:S:7 x_turn:T:11 residual:V:1,0 x_copy:S:6 stage2:T:0,0 x_copy:S:10 d_quant:V:2
x_copy:V:9 w_turn:T:1,0 x_copy:S:11 w_turn:T:1,3 w_turn:T:1,1 w_turn:T:1,4 d_quant:V:1 w_copy:S:1,3 w_turn:T:1,2
w_turn:T:1,5 x_quant:V:2 w_copy:S:1,1 d_turn:T:5 w_copy:S:1,2 residual:V:1,1 stage2:T:1,0 w_copy:S:1,5 w_copy:S:1,4
stage2:T:1,3 h_relu:S:0,0 d_scale:V:5 stage2:T:1,1 h_relu:S:1,0 w_copy:S:1,0 stage2:T:1,2 h_relu:S:1,1 stage2:T:2,1
w3_quant:V:0 h_relu:S:1,2 d_quant:V:3 stage2:T:2,3 h_relu:S:1,3 w3_quant:V:2 stage2:T:2,0 x_quant:V:3 h_relu:S:0,1
h_relu:S:2,1 h_lay:V:1 stage2:T:2,2 h_relu:S:2,0 stage2:T:0,1 h_relu:S:2,3 w3_quant:V:1 stage2:T:3,1 h_relu:S:2,2
h_quant:V:1 h_relu:S:0,3 stage2:T:3,0 h_lay:V:2 h_relu:S:0,2 stage3:T:4 h_lay:S:0 stage3:T:2 add:V:4,0,256
h_relu:S:3,0 stage3:T:5 h_quant:V:0 h_relu:S:3,2 h_quant:V:2 h_relu:S:3,1 stage3:T:1 h_relu:S:3,3 add:V:2,0,256
stage3:T:0 h_lay:S:3 add:V:1,0,256 stage3:T:3 add:V:0,0,256 stage3:T:6 add:V:5,0,256 finish:S:0,0,128,256 h_quant:V:3
stage3:T:7 add:V:3,0,256 finish:S:0,0,0,128 stage3:T:8 add:V:6,128,256 add:V:7,0,256 finish:S:0,1,0,128 stage3:T:11
add:V:8,0,256 finish:S:0,1,128,256 stage3:T:10 add:V:6,0,128 add:V:11,0,256 finish:S:1,0,192,256 stage3:T:9
add:V:10,0,256 finish:S:1,0,0,64 finish:S:1,0,64,128 add:V:9,128,256 finish:S:1,0,128,192 add:V:9,0,128
finish:S:1,1,192,256 finish:V:1,1,128,192 finish:V:1,1,64,128 finish:S:1,1,0,64
"""


def tile_dijetresnetblock_pa_kernel(tc, x, d_h1_bytes, d_h1_scale, d1, W2, b2, W3, b3, out):
    nc = tc.nc
    with ExitStack() as ctx:
        keep = ctx.enter_context(tc.tile_pool(name="keep", bufs=1))
        work = ctx.enter_context(tc.tile_pool(name="work", bufs=2))
        psum = ctx.enter_context(tc.psum_pool(name="psum", bufs=8))
        ctx.enter_context(tc.manual_schedule())
        rows = [slice(b * P, (b + 1) * P) for b in range(2)]

        def new_bank():
            bank = psum.tile([P, 512], F32, name="bank")
            return bank

        def copy(engine, out_ap, in_ap):
            if engine == "S":
                nc.scalar.copy(out=out_ap, in_=in_ap)
            else:
                nc.vector.tensor_copy(out=out_ap, in_=in_ap)

        w_raw = [[keep.tile([P, 2, ND * KW], BF16, name="w_raw%d_%d" % (i, n), tag="raw%d_%d" % (i, n)) for n in range(2)] for i in range(2)]
        w_src = [W2.rearrange("(m t) i k -> m t (i k)", t=4), W3.rearrange("(t m) i k -> m t (i k)", t=4)]
        x_raw = [keep.tile([P, ND * JETS], BF16, name="x_raw%d" % b) for b in range(2)]
        d_bytes = [keep.tile([P, ND * NP], U8, name="d_bytes%d" % b) for b in range(2)]
        d1_raw = [keep.tile([P, ND, NP], BF16, name="d1_raw%d" % b, tag="raw0_%d" % b) for b in range(2)]
        d_scale = keep.tile([P, 4], F32, name="d_scale")
        b2_raw = keep.tile([P, 4], BF16, name="b2_raw")
        b2_col = keep.tile([P, 4], F32, name="b2_col")
        b3_row = keep.tile([P, ND], BF16, name="b3_row")
        b3_all = keep.tile([P, ND], F32, name="b3_all")
        ones = keep.tile([P, P], BF16, name="ones")

        def load_w(i, o):
            nc.sync.dma_start(out=w_raw[i][o // 2][:, o % 2, :], in_=w_src[i][:, o, :])

        def load_x(b):
            nc.sync.dma_start(out=x_raw[b][:], in_=x[rows[b]].rearrange("b i j -> b (i j)"))

        def load_d(b):
            nc.sync.dma_start(out=d_bytes[b][:], in_=d_h1_bytes[rows[b]].rearrange("b i s -> b (i s)"))

        nc.vector.memset(b3_row[:], 0.0)
        nc.vector.memset(ones[:], 1.0)
        for c in range(2):
            cols = slice(c * ND * KW // 2, (c + 1) * ND * KW // 2)
            nc.sync.dma_start(out=w_raw[0][0][:, 0, cols], in_=w_src[0][:, 0, cols])
        load_d(0)
        nc.sync.dma_start(out=d_scale[:], in_=d_h1_scale.rearrange("o (p t) w -> p (o t w)", t=4))
        nc.sync.dma_start(out=b3_row[0:1, :], in_=b3.unsqueeze(0))
        for o in range(1, 4):
            load_w(0, o)
        load_x(0)
        nc.sync.dma_start(out=b2_raw[:], in_=b2.rearrange("(p t) -> p t", t=4))
        for o in range(4):
            load_w(1, o)
        load_d(1)
        nc.sync.dma_start(out=d1_raw[0][:], in_=d1[rows[0]])
        load_x(1)
        nc.sync.dma_start(out=d1_raw[1][:], in_=d1[rows[1]])

        ident = keep.tile([P, P], F32, name="ident")
        make_identity(nc, ident[:])
        warm = keep.tile([P, 1], F32, name="warm")
        nc.vector.memset(warm[:], 0.0)
        nc.scalar.activation(out=warm[:], in_=warm[:], func=RELU)
        nc.gpsimd.tensor_copy(out=b2_col[:], in_=b2_raw[:])

        w_sh = [[keep.tile([P, KW, 2, P, 2], BF16, name="w_sh%d_%d" % (i, o), tag="w_sh%d" % o) for o in range(4)] for i in range(2)]
        w2_g = keep.tile([P, 12, P, 2], F32, name="w2_g", tag="w2_g", align_bytes=64)
        w2_c = keep.tile([P, 12, P], U32, name="w2_c", align_bytes=64)
        w2_s = keep.tile([P, 12, P], U8, name="w2_s", align_bytes=64)
        w3_g = keep.tile([P, KW, ND, 2], F32, name="w3_g", align_bytes=64)
        w3_c = keep.tile([P, KW, ND], U32, name="w3_c", align_bytes=64)
        w3_s = keep.tile([P, KW, ND], U8, name="w3_s", align_bytes=64)
        banks = {}

        def w_shuffle(engine, i, o, p0, p1):
            src = w_raw[i][o // 2][:, o % 2, :].rearrange("m (p u e k) -> m u p k e", u=2, e=2, k=KW)[:, :, p0:p1]
            dst = w_sh[i][o][:].rearrange("m k u p e -> m u p k e")[:, :, p0:p1]
            if engine == "V":
                nc.vector.tensor_copy(out=dst, in_=src)
            else:
                for u in range(2):
                    nc.scalar.copy(out=dst[:, u], in_=src[:, u])

        def w_transpose(engine, i, j):
            bank = new_bank()
            view = bank[:].rearrange("p (n u m) -> p n u m", n=2, u=2)
            for n in range(2):
                o, k = PIECES[2 * j + n]
                for u in range(2):
                    nc.tensor.transpose(view[:, n, u, :], w_sh[i][o][:, k, u].rearrange("m p e -> m (p e)").bitcast(F32), ident[:])
            banks["w", i, j] = bank

        def w_copy(engine, i, j):
            src = banks["w", i, j][:].rearrange("p (n u m) -> p n m u", n=2, u=2)
            (oa, ka), (ob, kb) = PIECES[2 * j], PIECES[2 * j + 1]
            if i == 0:
                dst = w2_g[:, 2 * j : 2 * j + 2]
            elif oa == ob:
                dst = w3_g[:, ka : ka + 2, oa * P : (oa + 1) * P, :]
            else:
                dst = w3_g[:, ka, oa * P : (oa + 2) * P, :].rearrange("p (n m) u -> p n m u", n=2)
            copy(engine, dst, src)

        def w2_quantise(engine, j):
            g = slice(4 * j, 4 * j + 4)
            nc.vector.quantize_mx(
                out=w2_c[:, g, :].rearrange("p n m -> p (n m)").bitcast(FP8X4),
                scales=w2_s[:, g, :].rearrange("p n m -> p (n m)"),
                in_=w2_g[:, g, :, :].rearrange("p n m u -> p (n m u)").bitcast(BF16))

        def w3_quantise(engine, k):
            nc.vector.quantize_mx(out=w3_c[:, k, :].bitcast(FP8X4), scales=w3_s[:, k, :],
                                  in_=w3_g[:, k, :, :].rearrange("p m u -> p (m u)").bitcast(BF16))

        res = [[keep.tile([P, 3, HALF, 2], F32, name="res%d_%d" % (b, h), tag="res%d" % h if b == 0 else "raw1_%d" % h) for h in range(2)] for b in range(2)]

        def b3_spread(engine):
            bank = new_bank()
            nc.tensor.matmul(bank[:], lhsT=ones[:], rhs=b3_row[:], start=True, stop=True)
            banks["b3"] = bank

        def b3_copy(engine):
            copy(engine, b3_all[:], banks["b3"][:])

        def residual(engine, b, half):
            o = slice(half * HALF, (half + 1) * HALF)
            nc.vector.tensor_tensor(out=res[b][half][:], in0=d1_raw[b][:, o, :].rearrange("b o (g s) -> b g o s", s=2),
                                    in1=b3_all[:, o].unsqueeze(1).unsqueeze(3).to_broadcast([P, 3, HALF, 2]), op=ADD)

        x_c = [keep.tile([P, 2, z * P], U32, name="x_c%d" % q, align_bytes=64) for q, z in enumerate(GROUP_SIZES)]
        x_s = [keep.tile([P, 2, z * P], U8, name="x_s%d" % q, align_bytes=64) for q, z in enumerate(GROUP_SIZES)]
        d_c = [keep.tile([P, z * P], U32, name="d_c%d" % q, align_bytes=64) for q, z in enumerate(GROUP_SIZES)]
        d_s = [keep.tile([P, z * P], U8, name="d_s%d" % q, align_bytes=64) for q, z in enumerate(GROUP_SIZES)]
        h_c = [keep.tile([P, z * P], U32, name="h_c%d" % q, align_bytes=64) for q, z in enumerate(GROUP_SIZES)]
        h_s = [keep.tile([P, z * P], U8, name="h_s%d" % q, align_bytes=64) for q, z in enumerate(GROUP_SIZES)]
        x_g, d_g, h_p, h_g, acc2 = {}, {}, {}, {}, {}

        def x_transpose(engine, n):
            b, s = n // NP, n % NP
            bank = new_bank()
            words = x_raw[b][:].bitcast(F32).rearrange("b (p t s) -> b t s p", t=4, s=NP)
            for t in range(4):
                nc.tensor.transpose(bank[:, t * P : (t + 1) * P], words[:, t, s, :], ident[:])
            banks["x", n] = bank

        def x_copy(engine, n):
            q, r = GROUP_OF[n]
            if q not in x_g:
                x_g[q] = work.tile([P, 2, GROUP_SIZES[q] * P, 4], BF16, name="xg", align_bytes=64)
            copy(engine, x_g[q][:, :, r * P : (r + 1) * P, :], banks["x", n][:].bitcast(BF16).rearrange("p (t b k) -> p k b t", t=4, k=2))

        def x_quantise(engine, q):
            nc.vector.quantize_mx(out=x_c[q][:].rearrange("p k n -> p (k n)").bitcast(FP8X4),
                                  scales=x_s[q][:].rearrange("p k n -> p (k n)"),
                                  in_=x_g[q][:].rearrange("p k n t -> p (k n t)"))

        d_raw = [keep.tile([P, ND * NP], BF16, name="d_raw%d" % b) for b in range(2)]

        def d_widen(engine, b):
            copy(engine, d_raw[b][:], d_bytes[b][:].bitcast(FP8))

        def d_transpose(engine, pair):
            b, g = pair // 3, pair % 3
            words = d_raw[b][:].bitcast(F32).rearrange("b (p t g) -> b g t p", t=4, g=3)
            bank = new_bank()
            for t in range(4):
                nc.tensor.transpose(bank[:, t * P : (t + 1) * P], words[:, g, t, :], ident[:])
            banks["d", pair] = bank

        def d_multiply(engine, pair):
            q, r = GROUP_OF[2 * pair]
            if q not in d_g:
                d_g[q] = work.tile([P, GROUP_SIZES[q] * P, 4], BF16, name="dg", align_bytes=64)
            nc.vector.tensor_tensor(
                out=d_g[q][:, r * P : (r + 2) * P, :].rearrange("p (s b) t -> p s b t", s=2),
                in0=banks["d", pair][:].bitcast(BF16).rearrange("p (t b s) -> p s b t", t=4, s=2),
                in1=d_scale[:].unsqueeze(1).unsqueeze(1).to_broadcast([P, 2, P, 4]), op=MULT)

        def d_quantise(engine, q):
            nc.vector.quantize_mx(out=d_c[q][:].bitcast(FP8X4), scales=d_s[q][:], in_=d_g[q][:].rearrange("p n t -> p (n t)"))

        def first_stage(engine, q, a):
            width = GROUP_SIZES[q] * P
            bank = new_bank()
            for n in range(512 // width):
                t = (512 // width) * a + n
                acc2[q, t] = bank[:, n * width : (n + 1) * width]
                for k in range(KW):
                    g = PLACE_OF[t, k]
                    rhs, rhs_scale = (x_c[q][:, k], x_s[q][:, k]) if k < 2 else (d_c[q][:], d_s[q][:])
                    nc.tensor.matmul_mx(out=acc2[q, t], lhsT=w2_c[:, g, :].bitcast(FP8X4), lhsT_scale=w2_s[:, g, :],
                                        rhs=rhs.bitcast(FP8X4), rhs_scale=rhs_scale, start=(k == 0), stop=(k == 2))

        def h_relu(engine, q, t):
            if q not in h_p:
                h_p[q] = work.tile([P, 4, GROUP_SIZES[q] * P], BF16, name="hp", bufs=3)
            nc.scalar.activation(out=h_p[q][:, t, :], in_=acc2[q, t], func=RELU, bias=b2_col[:, t : t + 1])

        def h_interleave(engine, q):
            h_g[q] = work.tile([P, GROUP_SIZES[q] * P, 4], BF16, name="hg", bufs=3, align_bytes=64)
            copy(engine, h_g[q][:].rearrange("p (c i) t -> p c t i", i=4), h_p[q][:].rearrange("p t (c i) -> p c t i", i=4))

        def h_quantise(engine, q):
            nc.vector.quantize_mx(out=h_c[q][:].bitcast(FP8X4), scales=h_s[q][:], in_=h_g[q][:].rearrange("p n t -> p (n t)"))

        sums = [keep.tile([P, 2, 3, HALF, 2], F32, name="sums%d" % b, tag="sums" if b == 0 else "w2_g", align_bytes=64) for b in range(2)]
        result = [keep.tile([P, ND, NP], F32, name="result%d" % b, tag="result" if b == 0 else "x_raw0") for b in range(2)]

        def second_stage(engine, n):
            b, half, g = n // 6, (n % 6) // 3, n % 3
            o = slice(half * HALF, (half + 1) * HALF)
            bank = new_bank()
            for s in range(2):
                q, r = GROUP_OF[NP * b + 2 * g + s]
                c = slice(r * P, (r + 1) * P)
                for k in range(KW):
                    lhs, lhs_scale = (x_c[q][:, k, c], x_s[q][:, k, c]) if k < 2 else (h_c[q][:, c], h_s[q][:, c])
                    nc.tensor.matmul_mx(out=bank[:, s * HALF : (s + 1) * HALF], lhsT=lhs.bitcast(FP8X4), lhsT_scale=lhs_scale,
                                        rhs=w3_c[:, k, o].bitcast(FP8X4), rhs_scale=w3_s[:, k, o], start=(k == 0), stop=(k == 2))
            banks["out", n] = bank

        def add_residual(engine, n, o0, o1):
            b, half, g = n // 6, (n % 6) // 3, n % 3
            nc.vector.tensor_tensor(out=sums[b][:, half, g, o0:o1], in0=banks["out", n][:].rearrange("p (s o) -> p o s", s=2)[:, o0:o1],
                                    in1=res[b][half][:, g, o0:o1], op=ADD)

        def finish(engine, b, half, o0, o1):
            o = slice(half * HALF + o0, half * HALF + o1)
            dst = result[b][:, o, :].rearrange("p o (g s) -> p o g s", s=2)
            src = sums[b][:, half, :, o0:o1, :].rearrange("p g o s -> p o g s")
            if engine == "S":
                nc.scalar.activation(out=dst, in_=src, func=RELU)
            else:
                nc.vector.tensor_scalar_max(out=dst, in0=src, scalar1=0.0)
            nc.sync.dma_start(out=out[rows[b], o, :], in_=result[b][:, o, :])

        STEPS = {
            "w_shuffle": w_shuffle, "w_turn": w_transpose, "w_copy": w_copy, "w2_quant": w2_quantise, "w3_quant": w3_quantise,
            "b3_spread": b3_spread, "b3_copy": b3_copy, "residual": residual,
            "x_turn": x_transpose, "x_copy": x_copy, "x_quant": x_quantise,
            "d_widen": d_widen, "d_turn": d_transpose, "d_scale": d_multiply, "d_quant": d_quantise,
            "stage2": first_stage, "h_relu": h_relu, "h_lay": h_interleave, "h_quant": h_quantise,
            "stage3": second_stage, "add": add_residual, "finish": finish,
        }
        for entry in ORDER.split():
            name, engine, arguments = entry.split(":")
            STEPS[name](engine, *[int(v) for v in arguments.split(",") if v])
